import numpy as np
import ml_dtypes


def mxq(x, axis, fmt="e4m3"):
    dtype, down = {"e4m3": (ml_dtypes.float8_e4m3fn, 7), "e5m2": (ml_dtypes.float8_e5m2, 14)}[fmt]
    v = np.moveaxis(np.asarray(x, np.float32).astype(ml_dtypes.bfloat16).astype(np.float64), axis, -1)
    blocks = v.reshape(v.shape[:-1] + (-1, 32))
    amax = np.abs(blocks).max(-1, keepdims=True)
    byte = np.maximum(np.where(amax > 0, np.frexp(amax)[1] - 1 + 127, 0) - down, 1)
    scale = np.exp2(byte - 127.0)
    codes = (blocks / scale).astype(np.float32).astype(dtype).astype(np.float64)
    return np.moveaxis((codes * scale).reshape(v.shape), -1, axis)


WIDE = False


def mx_kscale(k):
    if not WIDE:
        return np.ones(k)
    levels = np.array([10, -10, 5, -5, 0])
    a = np.random.permutation(np.resize(levels, k // 512 * 4)).reshape(k // 512, 4)
    idx = np.arange(k)
    return np.exp2(a[idx // 512, idx % 128 // 32])


BF16 = ml_dtypes.bfloat16


def bf(x):
    return np.asarray(x, np.float32).astype(BF16)


def f64(x):
    return np.asarray(x).astype(np.float64)


E2M1 = np.array([0.0, 0.5, 1.0, 1.5, 2.0, 3.0, 4.0, 6.0, -0.0, -0.5, -1.0, -1.5, -2.0, -3.0, -4.0, -6.0])


def pack_weight(w, fmt):
    k, n = w.shape
    w = f64(bf(w)).reshape(k // 32, 32, n)
    amax = np.abs(w).max(1)
    if fmt == "e4m3":
        byte = np.frexp(amax)[1] - 1 + 127 - 7
    else:
        mant, ex = np.frexp(amax / 6.0)
        byte = np.where(mant > 0.5, ex, ex - 1) + 127
    byte = np.clip(np.where(amax > 0, byte, 1), 1, 254)
    scaled = (w * np.exp2(127.0 - byte)[:, None, :]).reshape(k, n).astype(np.float32)
    by_word = np.ascontiguousarray(scaled.reshape(k // 512, 128, 4, n).transpose(0, 1, 3, 2))
    if fmt == "e4m3":
        words = by_word.astype(ml_dtypes.float8_e4m3fn).view(np.uint8)
    else:
        c = by_word.astype(ml_dtypes.float4_e2m1fn).view(np.uint8) & 0xF
        words = c[..., 0::2] | (c[..., 1::2] << 4)
    return np.ascontiguousarray(words), np.ascontiguousarray(byte.astype(np.uint8).reshape(k // 512, 16, n))


def unpack_weight(words, scales, fmt):
    g, p, n, _ = words.shape
    if fmt == "e4m3":
        vals = np.ascontiguousarray(words).view(ml_dtypes.float8_e4m3fn).astype(np.float64)
    else:
        nib = np.empty((g, p, n, 4), np.uint8)
        nib[..., 0::2] = words & 0xF
        nib[..., 1::2] = words >> 4
        vals = E2M1[nib]
    vals = vals * np.repeat(np.exp2(scales.astype(np.float64) - 127.0), 8, axis=1)[..., None]
    return vals.transpose(0, 1, 3, 2).reshape(g * 512, n)


G, B, NF, T, I, R, H = 4, 512, 2048, 512, 512, 512, 512


def sigmoid(z):
    return 1.0 / (1.0 + np.exp(-z))


def setup_inputs():
    ki, kt, kh = mx_kscale(I), mx_kscale(T), mx_kscale(H)
    kw, ku = mx_kscale(R), mx_kscale(R)
    decoder_input = bf(np.random.standard_normal((B, I)) * ki)
    rnn_h = bf(np.random.standard_normal((B, H)) * kh)
    rnn_c = bf(np.random.standard_normal((B, H)))
    s = bf(np.random.standard_normal((B, T)) * kt)
    Wa = np.random.standard_normal((G, I, R)) / np.sqrt(I) / ki[:, None] * kw
    Wb = np.random.standard_normal((G, T, R)) / np.sqrt(T) / kt[:, None]
    Wc = np.random.standard_normal((G, R, H)) * 0.7 / np.sqrt(R) / kw[:, None]
    Ua = np.random.standard_normal((G, H, R)) / np.sqrt(H) / kh[:, None] * ku
    Ub = np.random.standard_normal((G, T, R)) / np.sqrt(T) / kt[:, None]
    Uc = np.random.standard_normal((G, R, H)) * 0.7 / np.sqrt(R) / ku[:, None]
    logits_v = bf(np.random.standard_normal((G, B, H)) * 0.7)
    b = bf(np.random.standard_normal((G, H)) * 0.2)
    Wa_words, Wa_scales = pack_weight(Wa.reshape(-1, R), "e4m3")
    Wb_words, Wb_scales = pack_weight(Wb.reshape(-1, R), "e4m3")
    Wc_words, Wc_scales = pack_weight(Wc.reshape(-1, H), "e4m3")
    Ua_words, Ua_scales = pack_weight(Ua.reshape(-1, R), "e4m3")
    Ub_words, Ub_scales = pack_weight(Ub.reshape(-1, R), "e4m3")
    Uc_words, Uc_scales = pack_weight(Uc.reshape(-1, H), "e4m3")
    return {"decoder_input": decoder_input,
            "rnn_h": rnn_h,
            "rnn_c": rnn_c,
            "s": s,
            "Wa_words": Wa_words, "Wa_scales": Wa_scales,
            "Wb_words": Wb_words, "Wb_scales": Wb_scales,
            "Wc_words": Wc_words, "Wc_scales": Wc_scales,
            "Ua_words": Ua_words, "Ua_scales": Ua_scales,
            "Ub_words": Ub_words, "Ub_scales": Ub_scales,
            "Uc_words": Uc_words, "Uc_scales": Uc_scales,
            "logits_v": logits_v,
            "b": b}


def reference(decoder_input, rnn_h, rnn_c, s, Wa_words, Wa_scales, Wb_words, Wb_scales, Wc_words, Wc_scales,
              Ua_words, Ua_scales, Ub_words, Ub_scales, Uc_words, Uc_scales, logits_v, b):
    sq = mxq(f64(s), 1, "e4m3")
    t2 = sq @ unpack_weight(Wb_words, Wb_scales, "e4m3").reshape(G, T, R)
    t1 = mxq(f64(decoder_input), 1, "e4m3") @ unpack_weight(Wa_words, Wa_scales, "e4m3").reshape(G, I, R)
    t5 = sq @ unpack_weight(Ub_words, Ub_scales, "e4m3").reshape(G, T, R)
    t6 = mxq(f64(rnn_h), 1, "e4m3") @ unpack_weight(Ua_words, Ua_scales, "e4m3").reshape(G, H, R)
    logits = ((mxq(t1 * t2, 2, "e4m3") @ unpack_weight(Wc_words, Wc_scales, "e4m3").reshape(G, R, H))
              + f64(logits_v)
              + (mxq(t5 * t6, 2, "e4m3") @ unpack_weight(Uc_words, Uc_scales, "e4m3").reshape(G, R, H))
              + f64(b)[:, None, :])
    i = sigmoid(logits[0])
    f = sigmoid(logits[1])
    o = sigmoid(logits[2])
    g = np.tanh(logits[3])
    new_c = f * f64(rnn_c) + i * g
    new_h = o * np.tanh(new_c)
    return new_h, new_c

@@ -1,0 +1,236 @@
+from contextlib import ExitStack
+
+import concourse.mybir as mybir
+from concourse.masks import make_identity
+
+FP8X4 = mybir.dt.float8_e4m3fn_x4
+BF16 = mybir.dt.bfloat16
+F32 = mybir.dt.float32
+I32 = mybir.dt.int32
+U32 = mybir.dt.uint32
+U8 = mybir.dt.uint8
+ACT = mybir.ActivationFunctionType
+ALU = mybir.AluOpType
+
+P = 128
+PACK = 4
+WIDTH = 512
+ROW_TILES = 4
+QUADRANTS = 4
+
+GATE_I, GATE_F, GATE_O, GATE_G = 0, 1, 2, 3
+GATE_ORDER = (GATE_F, GATE_I, GATE_G, GATE_O)
+UNITS = len(GATE_ORDER) * ROW_TILES
+
+WEIGHTS = ("Wb", "Ua", "Wa", "Ub", "Wc", "Uc")
+
+FLOPS = 2 * 6 * 4 * WIDTH * WIDTH * WIDTH
+
+
+def tile_vnclcell_pb_e_kernel(
+    tc,
+    decoder_input, rnn_h, rnn_c, s,
+    Wa_words, Wa_scales, Wb_words, Wb_scales, Wc_words, Wc_scales,
+    Ua_words, Ua_scales, Ub_words, Ub_scales, Uc_words, Uc_scales,
+    logits_v, b,
+    out_0, out_1,
+):
+    nc = tc.nc
+    words_dram = {"Wa": Wa_words, "Wb": Wb_words, "Wc": Wc_words, "Ua": Ua_words, "Ub": Ub_words, "Uc": Uc_words}
+    scales_dram = {"Wa": Wa_scales, "Wb": Wb_scales, "Wc": Wc_scales, "Ua": Ua_scales, "Ub": Ub_scales, "Uc": Uc_scales}
+    rows_dram = {"s": s, "x": decoder_input, "h": rnn_h}
+
+    def by_row_tile(matrix):
+        return matrix.rearrange("(p j) c -> p j c", j=ROW_TILES)
+
+    with ExitStack() as ctx:
+        ctx.enter_context(tc.manual_schedule())
+        keep = ctx.enter_context(tc.tile_pool(name="keep", bufs=1))
+        work = ctx.enter_context(tc.tile_pool(name="work", bufs=3))
+        first_psum = ctx.enter_context(tc.psum_pool(name="first_psum", bufs=4))
+        flip_psum = ctx.enter_context(tc.psum_pool(name="flip_psum", bufs=1))
+        logit_psum = ctx.enter_context(tc.psum_pool(name="logit_psum", bufs=2))
+
+        planes = keep.tile([P, len(WEIGHTS), WIDTH], U8, align_bytes=64)
+        nc.vector.memset(planes[:].bitcast(I32), 0)
+        warm_in = keep.tile([P, 1], F32)
+        warm_out = keep.tile([P, 1], F32)
+        nc.vector.memset(warm_in[:], 0.0)
+        ident_f32 = keep.tile([P, P], F32)
+        make_identity(nc, ident_f32[:])
+        ident_bf16 = keep.tile([P, P], BF16)
+        make_identity(nc, ident_bf16[:])
+
+        raw = {}
+        for name in ("s", "x", "h"):
+            raw[name] = keep.tile([P, ROW_TILES, WIDTH], BF16, name="raw_" + name)
+            nc.scalar.dma_start(out=raw[name][:], in_=by_row_tile(rows_dram[name]))
+        nc.scalar.activation(out=warm_out[:], in_=warm_in[:], func=ACT.Sigmoid)
+
+        for w, name in enumerate(WEIGHTS):
+            for quadrant in range(QUADRANTS):
+                nc.sync.dma_start(
+                    out=planes[32 * quadrant : 32 * quadrant + 16, w, :].bitcast(I32),
+                    in_=scales_dram[name][:, 4 * quadrant : 4 * quadrant + 4, :].bitcast(I32),
+                )
+
+        words = {}
+        for name in WEIGHTS:
+            words[name] = keep.tile([P, len(GATE_ORDER), WIDTH], U32, name="words_" + name, align_bytes=64)
+        visual = keep.tile([P, len(GATE_ORDER), ROW_TILES, WIDTH], BF16)
+        bias = keep.tile([P, len(GATE_ORDER), WIDTH], BF16)
+        cell = keep.tile([P, ROW_TILES, WIDTH], BF16)
+        for position, e in enumerate(GATE_ORDER):
+            for name in WEIGHTS:
+                nc.sync.dma_start(
+                    out=words[name][:, e, :].bitcast(I32),
+                    in_=words_dram[name][e].rearrange("p n t -> p (n t)").bitcast(I32),
+                )
+            if position == 0:
+                nc.sync.dma_start(
+                    out=bias[:].rearrange("p g c -> p (g c)"),
+                    in_=b.rearrange("g c -> (g c)").partition_broadcast(P),
+                )
+            nc.sync.dma_start(out=visual[:, e], in_=by_row_tile(logits_v[e]))
+            if position == 0:
+                nc.sync.dma_start(out=cell[:], in_=by_row_tile(rnn_c))
+
+        row_codes = {}
+        row_scales = {}
+        row_grouped = {}
+
+        def flip_rows(name):
+            row_grouped[name] = keep.tile([P, ROW_TILES, WIDTH], BF16, name="grouped_" + name, align_bytes=64)
+            for half in range(2):
+                flipped = first_psum.tile([P, 2, 2, P], F32, tag="first", name="flipped_" + name)
+                for jj in range(2):
+                    pairs = raw[name][:, 2 * half + jj, :].bitcast(F32)
+                    for u in range(2):
+                        nc.tensor.transpose(flipped[:, jj, u, :], pairs[:, u : WIDTH // 2 : 2], ident_f32[:])
+                target = row_grouped[name][:, 2 * half : 2 * half + 2, :].bitcast(F32)
+                target = target.rearrange("p jj (r u) -> p jj r u", u=2)
+                source = flipped[:].rearrange("p jj u r -> p jj r u")
+                if half == 0:
+                    nc.vector.tensor_copy(out=target, in_=source)
+                else:
+                    nc.scalar.copy(out=target, in_=source)
+
+        def quantise_rows(name):
+            row_codes[name] = keep.tile([P, ROW_TILES * P], U32, name="codes_" + name, align_bytes=64)
+            row_scales[name] = keep.tile([P, ROW_TILES * P], U8, name="scales_" + name, align_bytes=64)
+            nc.vector.quantize_mx(
+                out=row_codes[name][:].bitcast(FP8X4),
+                scales=row_scales[name][:],
+                in_=row_grouped[name][:].rearrange("p j c -> p (j c)"),
+            )
+
+        flip_rows("s")
+        flip_rows("x")
+        quantise_rows("s")
+        flip_rows("h")
+        quantise_rows("x")
+        quantise_rows("h")
+
+        forget_cell = keep.tile([P, ROW_TILES, WIDTH], F32)
+        input_gate = keep.tile([P, ROW_TILES, WIDTH], F32)
+        new_cell = keep.tile([P, ROW_TILES, WIDTH], F32)
+        addend = {}
+        product = {}
+        grouped = {}
+        codes = {}
+        scales = {}
+
+        def weight_operand(name, e):
+            return {
+                "rhs": words[name][:, e, :].bitcast(FP8X4),
+                "rhs_scale": planes[4 * e : P, WEIGHTS.index(name), :],
+            }
+
+        def first_matmul(rows, j, name, e):
+            acc = first_psum.tile([P, WIDTH], F32, tag="first", name="acc_" + name)
+            nc.tensor.matmul_mx(
+                out=acc[:],
+                lhsT=row_codes[rows][:, j * P : (j + 1) * P].bitcast(FP8X4),
+                lhsT_scale=row_scales[rows][:, j * P : (j + 1) * P],
+                start=True,
+                stop=True,
+                **weight_operand(name, e),
+            )
+            return acc[:].rearrange("p (c t) -> p t c", t=PACK)
+
+        def products(n):
+            e, j = GATE_ORDER[n // ROW_TILES], n % ROW_TILES
+            addend[n] = work.tile([P, WIDTH], F32, tag="addend", name="addend", bufs=6)
+            nc.gpsimd.tensor_tensor(out=addend[n][:], in0=visual[:, e, j, :], in1=bias[:, e, :], op=ALU.add)
+            copied = (first_matmul("s", j, "Wb", e), first_matmul("h", j, "Ua", e))
+            direct = (first_matmul("x", j, "Wa", e), first_matmul("s", j, "Ub", e))
+            product[n] = work.tile([P, 2, PACK, P], BF16, tag="product", name="product")
+            for branch in range(2):
+                factor = work.tile([P, PACK, P], F32, tag="factor%d" % branch, name="factor")
+                nc.scalar.copy(out=factor[:], in_=copied[branch])
+                nc.vector.tensor_tensor(out=product[n][:, branch], in0=direct[branch], in1=factor[:], op=ALU.mult)
+
+        def flip_products(n):
+            grouped[n] = work.tile([P, 2, P, PACK], BF16, tag="grouped", name="grouped", align_bytes=64)
+            flipped = []
+            for branch in range(2):
+                flipped.append(flip_psum.tile([P, PACK, P], BF16, tag="flip%d" % branch, name="flipped"))
+                for t in range(PACK):
+                    nc.tensor.transpose(flipped[branch][:, t, :], product[n][:, branch, t, :], ident_bf16[:])
+            nc.scalar.copy(out=grouped[n][:, 0], in_=flipped[0][:].rearrange("p t r -> p r t"))
+            nc.vector.tensor_copy(out=grouped[n][:, 1], in_=flipped[1][:].rearrange("p t r -> p r t"))
+
+        def quantise_products(n):
+            codes[n] = work.tile([P, 2 * P], U32, tag="codes", name="codes", align_bytes=64)
+            scales[n] = work.tile([P, 2 * P], U8, tag="scales", name="scales", align_bytes=64)
+            nc.vector.quantize_mx(
+                out=codes[n][:].bitcast(FP8X4),
+                scales=scales[n][:],
+                in_=grouped[n][:].rearrange("p a r t -> p (a r t)"),
+            )
+
+        def gate(n):
+            e, j = GATE_ORDER[n // ROW_TILES], n % ROW_TILES
+            logit = logit_psum.tile([P, WIDTH], F32, tag="logit", name="logit")
+            for branch, name in enumerate(("Wc", "Uc")):
+                nc.tensor.matmul_mx(
+                    out=logit[:],
+                    lhsT=codes[n][:, branch * P : (branch + 1) * P].bitcast(FP8X4),
+                    lhsT_scale=scales[n][:, branch * P : (branch + 1) * P],
+                    start=(branch == 0),
+                    stop=(branch == 1),
+                    **weight_operand(name, e),
+                )
+            total = work.tile([P, WIDTH], F32, tag="total", name="total")
+            nc.vector.tensor_tensor(out=total[:], in0=logit[:], in1=addend[n][:], op=ALU.add)
+            if e == GATE_F:
+                value = work.tile([P, WIDTH], F32, tag="value", name="value")
+                nc.scalar.activation(out=value[:], in_=total[:], func=ACT.Sigmoid)
+                nc.gpsimd.tensor_tensor(out=forget_cell[:, j, :], in0=value[:], in1=cell[:, j, :], op=ALU.mult)
+            elif e == GATE_I:
+                nc.scalar.activation(out=input_gate[:, j, :], in_=total[:], func=ACT.Sigmoid)
+            elif e == GATE_G:
+                value = work.tile([P, WIDTH], F32, tag="value", name="value")
+                nc.scalar.activation(out=value[:], in_=total[:], func=ACT.Tanh)
+                fresh = work.tile([P, WIDTH], F32, tag="fresh", name="fresh")
+                nc.gpsimd.tensor_tensor(out=fresh[:], in0=value[:], in1=input_gate[:, j, :], op=ALU.mult)
+                nc.gpsimd.tensor_tensor(out=new_cell[:, j, :], in0=fresh[:], in1=forget_cell[:, j, :], op=ALU.add)
+                nc.sync.dma_start(out=by_row_tile(out_1)[:, j, :], in_=new_cell[:, j, :])
+            else:
+                squashed = work.tile([P, WIDTH], F32, tag="squashed", name="squashed")
+                nc.scalar.activation(out=squashed[:], in_=new_cell[:, j, :], func=ACT.Tanh)
+                value = work.tile([P, WIDTH], F32, tag="value", name="value")
+                nc.scalar.activation(out=value[:], in_=total[:], func=ACT.Sigmoid)
+                hidden = work.tile([P, WIDTH], F32, tag="hidden", name="hidden")
+                nc.gpsimd.tensor_tensor(out=hidden[:], in0=value[:], in1=squashed[:], op=ALU.mult)
+                nc.sync.dma_start(out=by_row_tile(out_0)[:, j, :], in_=hidden[:])
+
+        for n in range(UNITS + 2):
+            if n < UNITS:
+                products(n)
+            if 1 <= n <= UNITS:
+                flip_products(n - 1)
+            if n >= 2:
+                gate(n - 2)
+            if 1 <= n <= UNITS:
+                quantise_products(n - 1)

@@ -134,6 +134,8 @@ def tile_vnclcell_pb_e_kernel(
         forget_cell = keep.tile([P, ROW_TILES, WIDTH], F32)
         input_gate = keep.tile([P, ROW_TILES, WIDTH], F32)
         new_cell = keep.tile([P, ROW_TILES, WIDTH], F32)
+        squashed = keep.tile([P, ROW_TILES, WIDTH], F32)
+        total = {}
         addend = {}
         product = {}
         grouped = {}
@@ -158,10 +160,13 @@ def tile_vnclcell_pb_e_kernel(
             )
             return acc[:].rearrange("p (c t) -> p t c", t=PACK)
 
+        def add_bias(n):
+            e, j = GATE_ORDER[n // ROW_TILES], n % ROW_TILES
+            addend[n] = work.tile([P, WIDTH], F32, tag="addend", name="addend", bufs=2 * ROW_TILES)
+            nc.gpsimd.tensor_tensor(out=addend[n][:], in0=visual[:, e, j, :], in1=bias[:, e, :], op=ALU.add)
+
         def products(n):
             e, j = GATE_ORDER[n // ROW_TILES], n % ROW_TILES
-            addend[n] = work.tile([P, WIDTH], F32, tag="addend", name="addend", bufs=6)
-            nc.gpsimd.tensor_tensor(out=addend[n][:], in0=visual[:, e, j, :], in1=bias[:, e, :], op=ALU.add)
             copied = (first_matmul("s", j, "Wb", e), first_matmul("h", j, "Ua", e))
             direct = (first_matmul("x", j, "Wa", e), first_matmul("s", j, "Ub", e))
             product[n] = work.tile([P, 2, PACK, P], BF16, tag="product", name="product")
@@ -178,7 +183,10 @@ def tile_vnclcell_pb_e_kernel(
                 for t in range(PACK):
                     nc.tensor.transpose(flipped[branch][:, t, :], product[n][:, branch, t, :], ident_bf16[:])
             nc.scalar.copy(out=grouped[n][:, 0], in_=flipped[0][:].rearrange("p t r -> p r t"))
-            nc.vector.tensor_copy(out=grouped[n][:, 1], in_=flipped[1][:].rearrange("p t r -> p r t"))
+            if n % 2 == 0:
+                nc.vector.tensor_copy(out=grouped[n][:, 1], in_=flipped[1][:].rearrange("p t r -> p r t"))
+            else:
+                nc.scalar.copy(out=grouped[n][:, 1], in_=flipped[1][:].rearrange("p t r -> p r t"))
 
         def quantise_products(n):
             codes[n] = work.tile([P, 2 * P], U32, tag="codes", name="codes", align_bytes=64)
@@ -189,7 +197,7 @@ def tile_vnclcell_pb_e_kernel(
                 in_=grouped[n][:].rearrange("p a r t -> p (a r t)"),
             )
 
-        def gate(n):
+        def logits(n):
             e, j = GATE_ORDER[n // ROW_TILES], n % ROW_TILES
             logit = logit_psum.tile([P, WIDTH], F32, tag="logit", name="logit")
             for branch, name in enumerate(("Wc", "Uc")):
@@ -201,36 +209,44 @@ def tile_vnclcell_pb_e_kernel(
                     stop=(branch == 1),
                     **weight_operand(name, e),
                 )
-            total = work.tile([P, WIDTH], F32, tag="total", name="total")
-            nc.vector.tensor_tensor(out=total[:], in0=logit[:], in1=addend[n][:], op=ALU.add)
+            total[n] = work.tile([P, WIDTH], F32, tag="total", name="total")
+            nc.vector.tensor_tensor(out=total[n][:], in0=logit[:], in1=addend[n][:], op=ALU.add)
+
+        def gate(n):
+            e, j = GATE_ORDER[n // ROW_TILES], n % ROW_TILES
             if e == GATE_F:
                 value = work.tile([P, WIDTH], F32, tag="value", name="value")
-                nc.scalar.activation(out=value[:], in_=total[:], func=ACT.Sigmoid)
+                nc.scalar.activation(out=value[:], in_=total[n][:], func=ACT.Sigmoid)
                 nc.gpsimd.tensor_tensor(out=forget_cell[:, j, :], in0=value[:], in1=cell[:, j, :], op=ALU.mult)
             elif e == GATE_I:
-                nc.scalar.activation(out=input_gate[:, j, :], in_=total[:], func=ACT.Sigmoid)
+                nc.scalar.activation(out=input_gate[:, j, :], in_=total[n][:], func=ACT.Sigmoid)
             elif e == GATE_G:
                 value = work.tile([P, WIDTH], F32, tag="value", name="value")
-                nc.scalar.activation(out=value[:], in_=total[:], func=ACT.Tanh)
+                nc.scalar.activation(out=value[:], in_=total[n][:], func=ACT.Tanh)
                 fresh = work.tile([P, WIDTH], F32, tag="fresh", name="fresh")
                 nc.gpsimd.tensor_tensor(out=fresh[:], in0=value[:], in1=input_gate[:, j, :], op=ALU.mult)
                 nc.gpsimd.tensor_tensor(out=new_cell[:, j, :], in0=fresh[:], in1=forget_cell[:, j, :], op=ALU.add)
                 nc.sync.dma_start(out=by_row_tile(out_1)[:, j, :], in_=new_cell[:, j, :])
             else:
-                squashed = work.tile([P, WIDTH], F32, tag="squashed", name="squashed")
-                nc.scalar.activation(out=squashed[:], in_=new_cell[:, j, :], func=ACT.Tanh)
+                nc.scalar.activation(out=squashed[:, j, :], in_=new_cell[:, j, :], func=ACT.Tanh)
                 value = work.tile([P, WIDTH], F32, tag="value", name="value")
-                nc.scalar.activation(out=value[:], in_=total[:], func=ACT.Sigmoid)
+                nc.scalar.activation(out=value[:], in_=total[n][:], func=ACT.Sigmoid)
                 hidden = work.tile([P, WIDTH], F32, tag="hidden", name="hidden")
-                nc.gpsimd.tensor_tensor(out=hidden[:], in0=value[:], in1=squashed[:], op=ALU.mult)
+                nc.gpsimd.tensor_tensor(out=hidden[:], in0=value[:], in1=squashed[:, j, :], op=ALU.mult)
                 nc.sync.dma_start(out=by_row_tile(out_0)[:, j, :], in_=hidden[:])
 
-        for n in range(UNITS + 2):
+        for n in range(ROW_TILES):
+            add_bias(n)
+        for n in range(UNITS + 3):
+            if n + ROW_TILES < UNITS:
+                add_bias(n + ROW_TILES)
             if n < UNITS:
                 products(n)
             if 1 <= n <= UNITS:
                 flip_products(n - 1)
-            if n >= 2:
-                gate(n - 2)
+            if 2 <= n <= UNITS + 1:
+                logits(n - 2)
+            if n >= 3:
+                gate(n - 3)
             if 1 <= n <= UNITS:
                 quantise_products(n - 1)

@@ -22,7 +22,10 @@ GATE_I, GATE_F, GATE_O, GATE_G = 0, 1, 2, 3
 GATE_ORDER = (GATE_F, GATE_I, GATE_G, GATE_O)
 UNITS = len(GATE_ORDER) * ROW_TILES
 
-WEIGHTS = ("Wb", "Ua", "Wa", "Ub", "Wc", "Uc")
+FIRST_WEIGHTS = ("Wb", "Ua", "Wa", "Ub")
+SECOND_WEIGHTS = ("Wc", "Uc")
+WEIGHTS = FIRST_WEIGHTS + SECOND_WEIGHTS
+ROWS = ("s", "h", "x")
 
 FLOPS = 2 * 6 * 4 * WIDTH * WIDTH * WIDTH
 
@@ -61,75 +64,77 @@ def tile_vnclcell_pb_e_kernel(
         ident_bf16 = keep.tile([P, P], BF16)
         make_identity(nc, ident_bf16[:])
 
-        raw = {}
-        for name in ("s", "x", "h"):
-            raw[name] = keep.tile([P, ROW_TILES, WIDTH], BF16, name="raw_" + name)
-            nc.scalar.dma_start(out=raw[name][:], in_=by_row_tile(rows_dram[name]))
         nc.scalar.activation(out=warm_out[:], in_=warm_in[:], func=ACT.Sigmoid)
 
-        for w, name in enumerate(WEIGHTS):
-            for quadrant in range(QUADRANTS):
-                nc.sync.dma_start(
-                    out=planes[32 * quadrant : 32 * quadrant + 16, w, :].bitcast(I32),
-                    in_=scales_dram[name][:, 4 * quadrant : 4 * quadrant + 4, :].bitcast(I32),
-                )
-
+        raw = keep.tile([P, ROW_TILES, len(ROWS), WIDTH], BF16)
         words = {}
         for name in WEIGHTS:
             words[name] = keep.tile([P, len(GATE_ORDER), WIDTH], U32, name="words_" + name, align_bytes=64)
         visual = keep.tile([P, len(GATE_ORDER), ROW_TILES, WIDTH], BF16)
         bias = keep.tile([P, len(GATE_ORDER), WIDTH], BF16)
         cell = keep.tile([P, ROW_TILES, WIDTH], BF16)
-        for position, e in enumerate(GATE_ORDER):
-            for name in WEIGHTS:
+
+        def load_rows(j):
+            for i, name in enumerate(ROWS):
+                nc.sync.dma_start(out=raw[:, j, i, :], in_=by_row_tile(rows_dram[name])[:, j, :])
+
+        def load_scales(names):
+            for name in names:
+                for quadrant in range(QUADRANTS):
+                    nc.sync.dma_start(
+                        out=planes[32 * quadrant : 32 * quadrant + 16, WEIGHTS.index(name), :].bitcast(I32),
+                        in_=scales_dram[name][:, 4 * quadrant : 4 * quadrant + 4, :].bitcast(I32),
+                    )
+
+        def load_words(names, e):
+            for name in names:
                 nc.sync.dma_start(
                     out=words[name][:, e, :].bitcast(I32),
                     in_=words_dram[name][e].rearrange("p n t -> p (n t)").bitcast(I32),
                 )
-            if position == 0:
-                nc.sync.dma_start(
-                    out=bias[:].rearrange("p g c -> p (g c)"),
-                    in_=b.rearrange("g c -> (g c)").partition_broadcast(P),
-                )
+
+        load_rows(0)
+        load_scales(FIRST_WEIGHTS)
+        load_words(FIRST_WEIGHTS, GATE_ORDER[0])
+        load_rows(1)
+        load_scales(SECOND_WEIGHTS)
+        load_words(SECOND_WEIGHTS, GATE_ORDER[0])
+        load_rows(2)
+        load_rows(3)
+        nc.sync.dma_start(
+            out=bias[:].rearrange("p g c -> p (g c)"),
+            in_=b.rearrange("g c -> (g c)").partition_broadcast(P),
+        )
+        nc.sync.dma_start(out=visual[:, GATE_ORDER[0]], in_=by_row_tile(logits_v[GATE_ORDER[0]]))
+        nc.sync.dma_start(out=cell[:], in_=by_row_tile(rnn_c))
+        for e in GATE_ORDER[1:]:
+            load_words(WEIGHTS, e)
             nc.sync.dma_start(out=visual[:, e], in_=by_row_tile(logits_v[e]))
-            if position == 0:
-                nc.sync.dma_start(out=cell[:], in_=by_row_tile(rnn_c))
 
-        row_codes = {}
-        row_scales = {}
-        row_grouped = {}
+        row_grouped = keep.tile([P, ROW_TILES, len(ROWS), WIDTH], BF16, align_bytes=64)
+        row_codes = keep.tile([P, ROW_TILES, len(ROWS), P], U32, align_bytes=64)
+        row_scales = keep.tile([P, ROW_TILES, len(ROWS), P], U8, align_bytes=64)
 
-        def flip_rows(name):
-            row_grouped[name] = keep.tile([P, ROW_TILES, WIDTH], BF16, name="grouped_" + name, align_bytes=64)
-            for half in range(2):
-                flipped = first_psum.tile([P, 2, 2, P], F32, tag="first", name="flipped_" + name)
-                for jj in range(2):
-                    pairs = raw[name][:, 2 * half + jj, :].bitcast(F32)
-                    for u in range(2):
-                        nc.tensor.transpose(flipped[:, jj, u, :], pairs[:, u : WIDTH // 2 : 2], ident_f32[:])
-                target = row_grouped[name][:, 2 * half : 2 * half + 2, :].bitcast(F32)
-                target = target.rearrange("p jj (r u) -> p jj r u", u=2)
-                source = flipped[:].rearrange("p jj u r -> p jj r u")
-                if half == 0:
+        def flip_rows(j):
+            for i in range(len(ROWS)):
+                flipped = first_psum.tile([P, 2, P], F32, tag="first", name="flipped_rows")
+                pairs = raw[:, j, i, :].bitcast(F32)
+                for u in range(2):
+                    nc.tensor.transpose(flipped[:, u, :], pairs[:, u : WIDTH // 2 : 2], ident_f32[:])
+                target = row_grouped[:, j, i, :].bitcast(F32).rearrange("p (r u) -> p r u", u=2)
+                source = flipped[:].rearrange("p u r -> p r u")
+                if i % 2 == 0:
                     nc.vector.tensor_copy(out=target, in_=source)
                 else:
                     nc.scalar.copy(out=target, in_=source)
 
-        def quantise_rows(name):
-            row_codes[name] = keep.tile([P, ROW_TILES * P], U32, name="codes_" + name, align_bytes=64)
-            row_scales[name] = keep.tile([P, ROW_TILES * P], U8, name="scales_" + name, align_bytes=64)
-            nc.vector.quantize_mx(
-                out=row_codes[name][:].bitcast(FP8X4),
-                scales=row_scales[name][:],
-                in_=row_grouped[name][:].rearrange("p j c -> p (j c)"),
-            )
-
-        flip_rows("s")
-        flip_rows("x")
-        quantise_rows("s")
-        flip_rows("h")
-        quantise_rows("x")
-        quantise_rows("h")
+        def quantise_rows(j):
+            for i in range(len(ROWS)):
+                nc.vector.quantize_mx(
+                    out=row_codes[:, j, i, :].bitcast(FP8X4),
+                    scales=row_scales[:, j, i, :],
+                    in_=row_grouped[:, j, i, :],
+                )
 
         forget_cell = keep.tile([P, ROW_TILES, WIDTH], F32)
         input_gate = keep.tile([P, ROW_TILES, WIDTH], F32)
@@ -152,8 +157,8 @@ def tile_vnclcell_pb_e_kernel(
             acc = first_psum.tile([P, WIDTH], F32, tag="first", name="acc_" + name)
             nc.tensor.matmul_mx(
                 out=acc[:],
-                lhsT=row_codes[rows][:, j * P : (j + 1) * P].bitcast(FP8X4),
-                lhsT_scale=row_scales[rows][:, j * P : (j + 1) * P],
+                lhsT=row_codes[:, j, ROWS.index(rows), :].bitcast(FP8X4),
+                lhsT_scale=row_scales[:, j, ROWS.index(rows), :],
                 start=True,
                 stop=True,
                 **weight_operand(name, e),
@@ -183,7 +188,7 @@ def tile_vnclcell_pb_e_kernel(
                 for t in range(PACK):
                     nc.tensor.transpose(flipped[branch][:, t, :], product[n][:, branch, t, :], ident_bf16[:])
             nc.scalar.copy(out=grouped[n][:, 0], in_=flipped[0][:].rearrange("p t r -> p r t"))
-            if n % 2 == 0:
+            if n % 2 == 1:
                 nc.vector.tensor_copy(out=grouped[n][:, 1], in_=flipped[1][:].rearrange("p t r -> p r t"))
             else:
                 nc.scalar.copy(out=grouped[n][:, 1], in_=flipped[1][:].rearrange("p t r -> p r t"))
@@ -232,9 +237,11 @@ def tile_vnclcell_pb_e_kernel(
                 value = work.tile([P, WIDTH], F32, tag="value", name="value")
                 nc.scalar.activation(out=value[:], in_=total[n][:], func=ACT.Sigmoid)
                 hidden = work.tile([P, WIDTH], F32, tag="hidden", name="hidden")
-                nc.gpsimd.tensor_tensor(out=hidden[:], in0=value[:], in1=squashed[:, j, :], op=ALU.mult)
+                nc.vector.tensor_tensor(out=hidden[:], in0=value[:], in1=squashed[:, j, :], op=ALU.mult)
                 nc.sync.dma_start(out=by_row_tile(out_0)[:, j, :], in_=hidden[:])
 
+        flip_rows(0)
+        quantise_rows(0)
         for n in range(ROW_TILES):
             add_bias(n)
         for n in range(UNITS + 3):
@@ -242,11 +249,15 @@ def tile_vnclcell_pb_e_kernel(
                 add_bias(n + ROW_TILES)
             if n < UNITS:
                 products(n)
+            if n + 1 < ROW_TILES:
+                flip_rows(n + 1)
             if 1 <= n <= UNITS:
                 flip_products(n - 1)
             if 2 <= n <= UNITS + 1:
                 logits(n - 2)
-            if n >= 3:
-                gate(n - 3)
+            if n + 1 < ROW_TILES:
+                quantise_rows(n + 1)
             if 1 <= n <= UNITS:
                 quantise_products(n - 1)
+            if n >= 3:
+                gate(n - 3)

@@ -22,10 +22,7 @@ GATE_I, GATE_F, GATE_O, GATE_G = 0, 1, 2, 3
 GATE_ORDER = (GATE_F, GATE_I, GATE_G, GATE_O)
 UNITS = len(GATE_ORDER) * ROW_TILES
 
-FIRST_WEIGHTS = ("Wb", "Ua", "Wa", "Ub")
-SECOND_WEIGHTS = ("Wc", "Uc")
-WEIGHTS = FIRST_WEIGHTS + SECOND_WEIGHTS
-ROWS = ("s", "h", "x")
+WEIGHTS = ("Wb", "Ua", "Wa", "Ub", "Wc", "Uc")
 
 FLOPS = 2 * 6 * 4 * WIDTH * WIDTH * WIDTH
 
@@ -64,77 +61,75 @@ def tile_vnclcell_pb_e_kernel(
         ident_bf16 = keep.tile([P, P], BF16)
         make_identity(nc, ident_bf16[:])
 
+        raw = {}
+        for name in ("s", "x", "h"):
+            raw[name] = keep.tile([P, ROW_TILES, WIDTH], BF16, name="raw_" + name)
+            nc.scalar.dma_start(out=raw[name][:], in_=by_row_tile(rows_dram[name]))
         nc.scalar.activation(out=warm_out[:], in_=warm_in[:], func=ACT.Sigmoid)
 
-        raw = keep.tile([P, ROW_TILES, len(ROWS), WIDTH], BF16)
+        for w, name in enumerate(WEIGHTS):
+            for quadrant in range(QUADRANTS):
+                nc.sync.dma_start(
+                    out=planes[32 * quadrant : 32 * quadrant + 16, w, :].bitcast(I32),
+                    in_=scales_dram[name][:, 4 * quadrant : 4 * quadrant + 4, :].bitcast(I32),
+                )
+
         words = {}
         for name in WEIGHTS:
             words[name] = keep.tile([P, len(GATE_ORDER), WIDTH], U32, name="words_" + name, align_bytes=64)
         visual = keep.tile([P, len(GATE_ORDER), ROW_TILES, WIDTH], BF16)
         bias = keep.tile([P, len(GATE_ORDER), WIDTH], BF16)
         cell = keep.tile([P, ROW_TILES, WIDTH], BF16)
-
-        def load_rows(j):
-            for i, name in enumerate(ROWS):
-                nc.sync.dma_start(out=raw[:, j, i, :], in_=by_row_tile(rows_dram[name])[:, j, :])
-
-        def load_scales(names):
-            for name in names:
-                for quadrant in range(QUADRANTS):
-                    nc.sync.dma_start(
-                        out=planes[32 * quadrant : 32 * quadrant + 16, WEIGHTS.index(name), :].bitcast(I32),
-                        in_=scales_dram[name][:, 4 * quadrant : 4 * quadrant + 4, :].bitcast(I32),
-                    )
-
-        def load_words(names, e):
-            for name in names:
+        for position, e in enumerate(GATE_ORDER):
+            for name in WEIGHTS:
                 nc.sync.dma_start(
                     out=words[name][:, e, :].bitcast(I32),
                     in_=words_dram[name][e].rearrange("p n t -> p (n t)").bitcast(I32),
                 )
-
-        load_rows(0)
-        load_scales(FIRST_WEIGHTS)
-        load_words(FIRST_WEIGHTS, GATE_ORDER[0])
-        load_rows(1)
-        load_scales(SECOND_WEIGHTS)
-        load_words(SECOND_WEIGHTS, GATE_ORDER[0])
-        load_rows(2)
-        load_rows(3)
-        nc.sync.dma_start(
-            out=bias[:].rearrange("p g c -> p (g c)"),
-            in_=b.rearrange("g c -> (g c)").partition_broadcast(P),
-        )
-        nc.sync.dma_start(out=visual[:, GATE_ORDER[0]], in_=by_row_tile(logits_v[GATE_ORDER[0]]))
-        nc.sync.dma_start(out=cell[:], in_=by_row_tile(rnn_c))
-        for e in GATE_ORDER[1:]:
-            load_words(WEIGHTS, e)
+            if position == 0:
+                nc.sync.dma_start(
+                    out=bias[:].rearrange("p g c -> p (g c)"),
+                    in_=b.rearrange("g c -> (g c)").partition_broadcast(P),
+                )
             nc.sync.dma_start(out=visual[:, e], in_=by_row_tile(logits_v[e]))
+            if position == 0:
+                nc.sync.dma_start(out=cell[:], in_=by_row_tile(rnn_c))
 
-        row_grouped = keep.tile([P, ROW_TILES, len(ROWS), WIDTH], BF16, align_bytes=64)
-        row_codes = keep.tile([P, ROW_TILES, len(ROWS), P], U32, align_bytes=64)
-        row_scales = keep.tile([P, ROW_TILES, len(ROWS), P], U8, align_bytes=64)
+        row_codes = {}
+        row_scales = {}
+        row_grouped = {}
 
-        def flip_rows(j):
-            for i in range(len(ROWS)):
-                flipped = first_psum.tile([P, 2, P], F32, tag="first", name="flipped_rows")
-                pairs = raw[:, j, i, :].bitcast(F32)
-                for u in range(2):
-                    nc.tensor.transpose(flipped[:, u, :], pairs[:, u : WIDTH // 2 : 2], ident_f32[:])
-                target = row_grouped[:, j, i, :].bitcast(F32).rearrange("p (r u) -> p r u", u=2)
-                source = flipped[:].rearrange("p u r -> p r u")
-                if i % 2 == 0:
+        def flip_rows(name):
+            row_grouped[name] = keep.tile([P, ROW_TILES, WIDTH], BF16, name="grouped_" + name, align_bytes=64)
+            for half in range(2):
+                flipped = first_psum.tile([P, 2, 2, P], F32, tag="first", name="flipped_" + name)
+                for jj in range(2):
+                    pairs = raw[name][:, 2 * half + jj, :].bitcast(F32)
+                    for u in range(2):
+                        nc.tensor.transpose(flipped[:, jj, u, :], pairs[:, u : WIDTH // 2 : 2], ident_f32[:])
+                target = row_grouped[name][:, 2 * half : 2 * half + 2, :].bitcast(F32)
+                target = target.rearrange("p jj (r u) -> p jj r u", u=2)
+                source = flipped[:].rearrange("p jj u r -> p jj r u")
+                if half == 0:
                     nc.vector.tensor_copy(out=target, in_=source)
                 else:
                     nc.scalar.copy(out=target, in_=source)
 
-        def quantise_rows(j):
-            for i in range(len(ROWS)):
-                nc.vector.quantize_mx(
-                    out=row_codes[:, j, i, :].bitcast(FP8X4),
-                    scales=row_scales[:, j, i, :],
-                    in_=row_grouped[:, j, i, :],
-                )
+        def quantise_rows(name):
+            row_codes[name] = keep.tile([P, ROW_TILES * P], U32, name="codes_" + name, align_bytes=64)
+            row_scales[name] = keep.tile([P, ROW_TILES * P], U8, name="scales_" + name, align_bytes=64)
+            nc.vector.quantize_mx(
+                out=row_codes[name][:].bitcast(FP8X4),
+                scales=row_scales[name][:],
+                in_=row_grouped[name][:].rearrange("p j c -> p (j c)"),
+            )
+
+        flip_rows("s")
+        flip_rows("x")
+        quantise_rows("s")
+        flip_rows("h")
+        quantise_rows("x")
+        quantise_rows("h")
 
         forget_cell = keep.tile([P, ROW_TILES, WIDTH], F32)
         input_gate = keep.tile([P, ROW_TILES, WIDTH], F32)
@@ -157,8 +152,8 @@ def tile_vnclcell_pb_e_kernel(
             acc = first_psum.tile([P, WIDTH], F32, tag="first", name="acc_" + name)
             nc.tensor.matmul_mx(
                 out=acc[:],
-                lhsT=row_codes[:, j, ROWS.index(rows), :].bitcast(FP8X4),
-                lhsT_scale=row_scales[:, j, ROWS.index(rows), :],
+                lhsT=row_codes[rows][:, j * P : (j + 1) * P].bitcast(FP8X4),
+                lhsT_scale=row_scales[rows][:, j * P : (j + 1) * P],
                 start=True,
                 stop=True,
                 **weight_operand(name, e),
@@ -181,25 +176,27 @@ def tile_vnclcell_pb_e_kernel(
                 nc.vector.tensor_tensor(out=product[n][:, branch], in0=direct[branch], in1=factor[:], op=ALU.mult)
 
         def flip_products(n):
-            grouped[n] = work.tile([P, 2, P, PACK], BF16, tag="grouped", name="grouped", align_bytes=64)
+            pair, half = n // 2, n % 2
+            if half == 0:
+                grouped[pair] = work.tile([P, 2, 2, P, PACK], BF16, tag="grouped", name="grouped", align_bytes=64)
             flipped = []
             for branch in range(2):
                 flipped.append(flip_psum.tile([P, PACK, P], BF16, tag="flip%d" % branch, name="flipped"))
                 for t in range(PACK):
                     nc.tensor.transpose(flipped[branch][:, t, :], product[n][:, branch, t, :], ident_bf16[:])
-            nc.scalar.copy(out=grouped[n][:, 0], in_=flipped[0][:].rearrange("p t r -> p r t"))
-            if n % 2 == 1:
-                nc.vector.tensor_copy(out=grouped[n][:, 1], in_=flipped[1][:].rearrange("p t r -> p r t"))
+            nc.scalar.copy(out=grouped[pair][:, half, 0], in_=flipped[0][:].rearrange("p t r -> p r t"))
+            if half == 0:
+                nc.vector.tensor_copy(out=grouped[pair][:, half, 1], in_=flipped[1][:].rearrange("p t r -> p r t"))
             else:
-                nc.scalar.copy(out=grouped[n][:, 1], in_=flipped[1][:].rearrange("p t r -> p r t"))
+                nc.scalar.copy(out=grouped[pair][:, half, 1], in_=flipped[1][:].rearrange("p t r -> p r t"))
 
-        def quantise_products(n):
-            codes[n] = work.tile([P, 2 * P], U32, tag="codes", name="codes", align_bytes=64)
-            scales[n] = work.tile([P, 2 * P], U8, tag="scales", name="scales", align_bytes=64)
+        def quantise_products(pair):
+            codes[pair] = work.tile([P, 2, 2, P], U32, tag="codes", name="codes", align_bytes=64)
+            scales[pair] = work.tile([P, 2, 2, P], U8, tag="scales", name="scales", align_bytes=64)
             nc.vector.quantize_mx(
-                out=codes[n][:].bitcast(FP8X4),
-                scales=scales[n][:],
-                in_=grouped[n][:].rearrange("p a r t -> p (a r t)"),
+                out=codes[pair][:].rearrange("p h a r -> p (h a r)").bitcast(FP8X4),
+                scales=scales[pair][:].rearrange("p h a r -> p (h a r)"),
+                in_=grouped[pair][:].rearrange("p h a r t -> p (h a r t)"),
             )
 
         def logits(n):
@@ -208,8 +205,8 @@ def tile_vnclcell_pb_e_kernel(
             for branch, name in enumerate(("Wc", "Uc")):
                 nc.tensor.matmul_mx(
                     out=logit[:],
-                    lhsT=codes[n][:, branch * P : (branch + 1) * P].bitcast(FP8X4),
-                    lhsT_scale=scales[n][:, branch * P : (branch + 1) * P],
+                    lhsT=codes[n // 2][:, n % 2, branch, :].bitcast(FP8X4),
+                    lhsT_scale=scales[n // 2][:, n % 2, branch, :],
                     start=(branch == 0),
                     stop=(branch == 1),
                     **weight_operand(name, e),
@@ -240,24 +237,18 @@ def tile_vnclcell_pb_e_kernel(
                 nc.vector.tensor_tensor(out=hidden[:], in0=value[:], in1=squashed[:, j, :], op=ALU.mult)
                 nc.sync.dma_start(out=by_row_tile(out_0)[:, j, :], in_=hidden[:])
 
-        flip_rows(0)
-        quantise_rows(0)
         for n in range(ROW_TILES):
             add_bias(n)
-        for n in range(UNITS + 3):
+        for n in range(UNITS + 4):
             if n + ROW_TILES < UNITS:
                 add_bias(n + ROW_TILES)
             if n < UNITS:
                 products(n)
-            if n + 1 < ROW_TILES:
-                flip_rows(n + 1)
             if 1 <= n <= UNITS:
                 flip_products(n - 1)
-            if 2 <= n <= UNITS + 1:
-                logits(n - 2)
-            if n + 1 < ROW_TILES:
-                quantise_rows(n + 1)
-            if 1 <= n <= UNITS:
-                quantise_products(n - 1)
-            if n >= 3:
-                gate(n - 3)
+            if 3 <= n <= UNITS + 2:
+                logits(n - 3)
+            if 2 <= n <= UNITS and n % 2 == 0:
+                quantise_products(n // 2 - 1)
+            if n >= 4:
+                gate(n - 4)

@@ -53,6 +53,11 @@ def tile_vnclcell_pb_e_kernel(
 
         planes = keep.tile([P, len(WEIGHTS), WIDTH], U8, align_bytes=64)
         nc.vector.memset(planes[:].bitcast(I32), 0)
+        bias_row = keep.tile([P, len(GATE_ORDER), WIDTH], BF16)
+        nc.vector.memset(bias_row[:], 0.0)
+        first_row_ones = keep.tile([P, P], BF16)
+        nc.vector.memset(first_row_ones[:], 0.0)
+        nc.vector.memset(first_row_ones[0:1, :], 1.0)
         warm_in = keep.tile([P, 1], F32)
         warm_out = keep.tile([P, 1], F32)
         nc.vector.memset(warm_in[:], 0.0)
@@ -66,6 +71,10 @@ def tile_vnclcell_pb_e_kernel(
             raw[name] = keep.tile([P, ROW_TILES, WIDTH], BF16, name="raw_" + name)
             nc.scalar.dma_start(out=raw[name][:], in_=by_row_tile(rows_dram[name]))
         nc.scalar.activation(out=warm_out[:], in_=warm_in[:], func=ACT.Sigmoid)
+        nc.scalar.dma_start(
+            out=bias_row[0:1].rearrange("p g c -> p (g c)"),
+            in_=b.rearrange("g c -> (g c)").unsqueeze(0),
+        )
 
         for w, name in enumerate(WEIGHTS):
             for quadrant in range(QUADRANTS):
@@ -85,11 +94,6 @@ def tile_vnclcell_pb_e_kernel(
                 nc.sync.dma_start(
                     out=words[name][:, e, :].bitcast(I32),
                     in_=words_dram[name][e].rearrange("p n t -> p (n t)").bitcast(I32),
-                )
-            if position == 0:
-                nc.sync.dma_start(
-                    out=bias[:].rearrange("p g c -> p (g c)"),
-                    in_=b.rearrange("g c -> (g c)").partition_broadcast(P),
                 )
             nc.sync.dma_start(out=visual[:, e], in_=by_row_tile(logits_v[e]))
             if position == 0:
@@ -127,6 +131,13 @@ def tile_vnclcell_pb_e_kernel(
         flip_rows("s")
         flip_rows("x")
         quantise_rows("s")
+        for e in range(len(GATE_ORDER)):
+            spread = first_psum.tile([P, WIDTH], F32, tag="first", name="spread")
+            nc.tensor.matmul(out=spread[:], lhsT=first_row_ones[:], rhs=bias_row[:, e, :], start=True, stop=True)
+            if e % 2 == 0:
+                nc.vector.tensor_copy(out=bias[:, e, :], in_=spread[:])
+            else:
+                nc.scalar.copy(out=bias[:, e, :], in_=spread[:])
         flip_rows("h")
         quantise_rows("x")
         quantise_rows("h")

@@ -22,7 +22,7 @@ GATE_I, GATE_F, GATE_O, GATE_G = 0, 1, 2, 3
 GATE_ORDER = (GATE_F, GATE_I, GATE_G, GATE_O)
 UNITS = len(GATE_ORDER) * ROW_TILES
 
-WEIGHTS = ("Wb", "Ua", "Wa", "Ub", "Wc", "Uc")
+WEIGHTS = ("Wb", "Wa", "Ua", "Ub", "Wc", "Uc")
 
 FLOPS = 2 * 6 * 4 * WIDTH * WIDTH * WIDTH
 
@@ -69,35 +69,48 @@ def tile_vnclcell_pb_e_kernel(
         raw = {}
         for name in ("s", "x", "h"):
             raw[name] = keep.tile([P, ROW_TILES, WIDTH], BF16, name="raw_" + name)
-            nc.scalar.dma_start(out=raw[name][:], in_=by_row_tile(rows_dram[name]))
-        nc.scalar.activation(out=warm_out[:], in_=warm_in[:], func=ACT.Sigmoid)
-        nc.scalar.dma_start(
-            out=bias_row[0:1].rearrange("p g c -> p (g c)"),
-            in_=b.rearrange("g c -> (g c)").unsqueeze(0),
-        )
-
-        for w, name in enumerate(WEIGHTS):
-            for quadrant in range(QUADRANTS):
-                nc.sync.dma_start(
-                    out=planes[32 * quadrant : 32 * quadrant + 16, w, :].bitcast(I32),
-                    in_=scales_dram[name][:, 4 * quadrant : 4 * quadrant + 4, :].bitcast(I32),
-                )
-
         words = {}
         for name in WEIGHTS:
             words[name] = keep.tile([P, len(GATE_ORDER), WIDTH], U32, name="words_" + name, align_bytes=64)
         visual = keep.tile([P, len(GATE_ORDER), ROW_TILES, WIDTH], BF16)
         bias = keep.tile([P, len(GATE_ORDER), WIDTH], BF16)
         cell = keep.tile([P, ROW_TILES, WIDTH], BF16)
-        for position, e in enumerate(GATE_ORDER):
-            for name in WEIGHTS:
+
+        def load_rows(queue, name):
+            queue.dma_start(out=raw[name][:], in_=by_row_tile(rows_dram[name]))
+
+        def load_plane(name):
+            for quadrant in range(QUADRANTS):
                 nc.sync.dma_start(
-                    out=words[name][:, e, :].bitcast(I32),
-                    in_=words_dram[name][e].rearrange("p n t -> p (n t)").bitcast(I32),
+                    out=planes[32 * quadrant : 32 * quadrant + 16, WEIGHTS.index(name), :].bitcast(I32),
+                    in_=scales_dram[name][:, 4 * quadrant : 4 * quadrant + 4, :].bitcast(I32),
                 )
+
+        def load_words(name, e):
+            nc.sync.dma_start(
+                out=words[name][:, e, :].bitcast(I32),
+                in_=words_dram[name][e].rearrange("p n t -> p (n t)").bitcast(I32),
+            )
+
+        load_rows(nc.scalar, "s")
+        load_rows(nc.scalar, "x")
+        nc.scalar.activation(out=warm_out[:], in_=warm_in[:], func=ACT.Sigmoid)
+        nc.scalar.dma_start(
+            out=bias_row[0:1].rearrange("p g c -> p (g c)"),
+            in_=b.rearrange("g c -> (g c)").unsqueeze(0),
+        )
+        for name in WEIGHTS:
+            if name == "Ua":
+                load_rows(nc.sync, "h")
+            if name == "Wc":
+                nc.sync.dma_start(out=visual[:, GATE_ORDER[0]], in_=by_row_tile(logits_v[GATE_ORDER[0]]))
+            load_plane(name)
+            load_words(name, GATE_ORDER[0])
+        nc.sync.dma_start(out=cell[:], in_=by_row_tile(rnn_c))
+        for e in GATE_ORDER[1:]:
+            for name in WEIGHTS:
+                load_words(name, e)
             nc.sync.dma_start(out=visual[:, e], in_=by_row_tile(logits_v[e]))
-            if position == 0:
-                nc.sync.dma_start(out=cell[:], in_=by_row_tile(rnn_c))
 
         row_codes = {}
         row_scales = {}
@@ -128,18 +141,23 @@ def tile_vnclcell_pb_e_kernel(
                 in_=row_grouped[name][:].rearrange("p j c -> p (j c)"),
             )
 
-        flip_rows("s")
-        flip_rows("x")
-        quantise_rows("s")
-        for e in range(len(GATE_ORDER)):
+        def spread_bias(e):
             spread = first_psum.tile([P, WIDTH], F32, tag="first", name="spread")
             nc.tensor.matmul(out=spread[:], lhsT=first_row_ones[:], rhs=bias_row[:, e, :], start=True, stop=True)
             if e % 2 == 0:
                 nc.vector.tensor_copy(out=bias[:, e, :], in_=spread[:])
             else:
                 nc.scalar.copy(out=bias[:, e, :], in_=spread[:])
-        flip_rows("h")
+
+        flip_rows("s")
+        flip_rows("x")
+        quantise_rows("s")
+        spread_bias(0)
+        spread_bias(1)
         quantise_rows("x")
+        spread_bias(2)
+        spread_bias(3)
+        flip_rows("h")
         quantise_rows("h")
 
         forget_cell = keep.tile([P, ROW_TILES, WIDTH], F32)
@@ -178,13 +196,13 @@ def tile_vnclcell_pb_e_kernel(
 
         def products(n):
             e, j = GATE_ORDER[n // ROW_TILES], n % ROW_TILES
-            copied = (first_matmul("s", j, "Wb", e), first_matmul("h", j, "Ua", e))
-            direct = (first_matmul("x", j, "Wa", e), first_matmul("s", j, "Ub", e))
             product[n] = work.tile([P, 2, PACK, P], BF16, tag="product", name="product")
-            for branch in range(2):
+            for branch, (copied, direct) in enumerate(((("s", "Wb"), ("x", "Wa")), (("h", "Ua"), ("s", "Ub")))):
+                copied_acc = first_matmul(copied[0], j, copied[1], e)
+                direct_acc = first_matmul(direct[0], j, direct[1], e)
                 factor = work.tile([P, PACK, P], F32, tag="factor%d" % branch, name="factor")
-                nc.scalar.copy(out=factor[:], in_=copied[branch])
-                nc.vector.tensor_tensor(out=product[n][:, branch], in0=direct[branch], in1=factor[:], op=ALU.mult)
+                nc.scalar.copy(out=factor[:], in_=copied_acc)
+                nc.vector.tensor_tensor(out=product[n][:, branch], in0=direct_acc, in1=factor[:], op=ALU.mult)
 
         def flip_products(n):
             pair, half = n // 2, n % 2

@@ -48,7 +48,7 @@ def tile_vnclcell_pb_e_kernel(
         keep = ctx.enter_context(tc.tile_pool(name="keep", bufs=1))
         work = ctx.enter_context(tc.tile_pool(name="work", bufs=3))
         first_psum = ctx.enter_context(tc.psum_pool(name="first_psum", bufs=4))
-        flip_psum = ctx.enter_context(tc.psum_pool(name="flip_psum", bufs=1))
+        flip_psum = ctx.enter_context(tc.psum_pool(name="flip_psum", bufs=2))
         logit_psum = ctx.enter_context(tc.psum_pool(name="logit_psum", bufs=2))
 
         planes = keep.tile([P, len(WEIGHTS), WIDTH], U8, align_bytes=64)
@@ -63,8 +63,6 @@ def tile_vnclcell_pb_e_kernel(
         nc.vector.memset(warm_in[:], 0.0)
         ident_f32 = keep.tile([P, P], F32)
         make_identity(nc, ident_f32[:])
-        ident_bf16 = keep.tile([P, P], BF16)
-        make_identity(nc, ident_bf16[:])
 
         raw = {}
         for name in ("s", "x", "h"):
@@ -187,7 +185,7 @@ def tile_vnclcell_pb_e_kernel(
                 stop=True,
                 **weight_operand(name, e),
             )
-            return acc[:].rearrange("p (c t) -> p t c", t=PACK)
+            return acc[:].rearrange("p (c u e) -> p u c e", u=2, e=2)
 
         def add_bias(n):
             e, j = GATE_ORDER[n // ROW_TILES], n % ROW_TILES
@@ -196,11 +194,11 @@ def tile_vnclcell_pb_e_kernel(
 
         def products(n):
             e, j = GATE_ORDER[n // ROW_TILES], n % ROW_TILES
-            product[n] = work.tile([P, 2, PACK, P], BF16, tag="product", name="product")
+            product[n] = work.tile([P, 2, 2, P, 2], BF16, tag="product", name="product")
             for branch, (copied, direct) in enumerate(((("s", "Wb"), ("x", "Wa")), (("h", "Ua"), ("s", "Ub")))):
                 copied_acc = first_matmul(copied[0], j, copied[1], e)
                 direct_acc = first_matmul(direct[0], j, direct[1], e)
-                factor = work.tile([P, PACK, P], F32, tag="factor%d" % branch, name="factor")
+                factor = work.tile([P, 2, P, 2], F32, tag="factor%d" % branch, name="factor")
                 nc.scalar.copy(out=factor[:], in_=copied_acc)
                 nc.vector.tensor_tensor(out=product[n][:, branch], in0=direct_acc, in1=factor[:], op=ALU.mult)
 
@@ -208,16 +206,18 @@ def tile_vnclcell_pb_e_kernel(
             pair, half = n // 2, n % 2
             if half == 0:
                 grouped[pair] = work.tile([P, 2, 2, P, PACK], BF16, tag="grouped", name="grouped", align_bytes=64)
-            flipped = []
+            flipped = flip_psum.tile([P, 2, 2, P], F32, tag="flip", name="flipped")
             for branch in range(2):
-                flipped.append(flip_psum.tile([P, PACK, P], BF16, tag="flip%d" % branch, name="flipped"))
-                for t in range(PACK):
-                    nc.tensor.transpose(flipped[branch][:, t, :], product[n][:, branch, t, :], ident_bf16[:])
-            nc.scalar.copy(out=grouped[pair][:, half, 0], in_=flipped[0][:].rearrange("p t r -> p r t"))
-            if half == 0:
-                nc.vector.tensor_copy(out=grouped[pair][:, half, 1], in_=flipped[1][:].rearrange("p t r -> p r t"))
+                for u in range(2):
+                    pairs = product[n][:, branch, u].rearrange("p c e -> p (c e)").bitcast(F32)
+                    nc.tensor.transpose(flipped[:, branch, u, :], pairs, ident_f32[:])
+            target = grouped[pair][:, half].rearrange("p a r t -> p a (r t)").bitcast(F32)
+            target = target.rearrange("p a (r u) -> p a r u", u=2)
+            source = flipped[:].rearrange("p a u r -> p a r u")
+            if n % 4 == 0:
+                nc.vector.tensor_copy(out=target, in_=source)
             else:
-                nc.scalar.copy(out=grouped[pair][:, half, 1], in_=flipped[1][:].rearrange("p t r -> p r t"))
+                nc.scalar.copy(out=target, in_=source)
 
         def quantise_products(pair):
             codes[pair] = work.tile([P, 2, 2, P], U32, tag="codes", name="codes", align_bytes=64)

@@ -48,7 +48,8 @@ def tile_vnclcell_pb_e_kernel(
         keep = ctx.enter_context(tc.tile_pool(name="keep", bufs=1))
         work = ctx.enter_context(tc.tile_pool(name="work", bufs=3))
         first_psum = ctx.enter_context(tc.psum_pool(name="first_psum", bufs=4))
-        flip_psum = ctx.enter_context(tc.psum_pool(name="flip_psum", bufs=2))
+        flip_psum = ctx.enter_context(tc.psum_pool(name="flip_psum", bufs=1))
+        addend_psum = ctx.enter_context(tc.psum_pool(name="addend_psum", bufs=1))
         logit_psum = ctx.enter_context(tc.psum_pool(name="logit_psum", bufs=2))
 
         planes = keep.tile([P, len(WEIGHTS), WIDTH], U8, align_bytes=64)
@@ -63,6 +64,8 @@ def tile_vnclcell_pb_e_kernel(
         nc.vector.memset(warm_in[:], 0.0)
         ident_f32 = keep.tile([P, P], F32)
         make_identity(nc, ident_f32[:])
+        ident_bf16 = keep.tile([P, P], BF16)
+        make_identity(nc, ident_bf16[:])
 
         raw = {}
         for name in ("s", "x", "h"):
@@ -187,10 +190,18 @@ def tile_vnclcell_pb_e_kernel(
             )
             return acc[:].rearrange("p (c u e) -> p u c e", u=2, e=2)
 
-        def add_bias(n):
+        def add_bias_gpsimd(n):
             e, j = GATE_ORDER[n // ROW_TILES], n % ROW_TILES
-            addend[n] = work.tile([P, WIDTH], F32, tag="addend", name="addend", bufs=2 * ROW_TILES)
+            addend[n] = work.tile([P, WIDTH], F32, tag="addend_gpsimd", name="addend", bufs=ROW_TILES)
             nc.gpsimd.tensor_tensor(out=addend[n][:], in0=visual[:, e, j, :], in1=bias[:, e, :], op=ALU.add)
+
+        def add_bias_tensor(n):
+            e, j = GATE_ORDER[n // ROW_TILES], n % ROW_TILES
+            summed = addend_psum.tile([P, WIDTH], F32, tag="summed", name="summed")
+            nc.tensor.matmul(out=summed[:], lhsT=ident_bf16[:], rhs=visual[:, e, j, :], start=True, stop=False)
+            nc.tensor.matmul(out=summed[:], lhsT=first_row_ones[:], rhs=bias_row[:, e, :], start=False, stop=True)
+            addend[n] = work.tile([P, WIDTH], F32, tag="addend_tensor", name="addend", bufs=2)
+            nc.scalar.copy(out=addend[n][:], in_=summed[:])
 
         def products(n):
             e, j = GATE_ORDER[n // ROW_TILES], n % ROW_TILES
@@ -266,13 +277,15 @@ def tile_vnclcell_pb_e_kernel(
                 nc.vector.tensor_tensor(out=hidden[:], in0=value[:], in1=squashed[:, j, :], op=ALU.mult)
                 nc.sync.dma_start(out=by_row_tile(out_0)[:, j, :], in_=hidden[:])
 
-        for n in range(ROW_TILES):
-            add_bias(n)
+        for n in range(0, ROW_TILES, 2):
+            add_bias_gpsimd(n)
         for n in range(UNITS + 4):
-            if n + ROW_TILES < UNITS:
-                add_bias(n + ROW_TILES)
+            if n + ROW_TILES < UNITS and n % 2 == 0:
+                add_bias_gpsimd(n + ROW_TILES)
             if n < UNITS:
                 products(n)
+            if 3 <= n <= UNITS + 1 and n % 2 == 1:
+                add_bias_tensor(n - 2)
             if 1 <= n <= UNITS:
                 flip_products(n - 1)
             if 3 <= n <= UNITS + 2:

@@ -201,7 +201,10 @@ def tile_vnclcell_pb_e_kernel(
             nc.tensor.matmul(out=summed[:], lhsT=ident_bf16[:], rhs=visual[:, e, j, :], start=True, stop=False)
             nc.tensor.matmul(out=summed[:], lhsT=first_row_ones[:], rhs=bias_row[:, e, :], start=False, stop=True)
             addend[n] = work.tile([P, WIDTH], F32, tag="addend_tensor", name="addend", bufs=2)
-            nc.scalar.copy(out=addend[n][:], in_=summed[:])
+            if n % 4 == 1:
+                nc.vector.tensor_copy(out=addend[n][:], in_=summed[:])
+            else:
+                nc.scalar.copy(out=addend[n][:], in_=summed[:])
 
         def products(n):
             e, j = GATE_ORDER[n // ROW_TILES], n % ROW_TILES
@@ -230,13 +233,14 @@ def tile_vnclcell_pb_e_kernel(
             else:
                 nc.scalar.copy(out=target, in_=source)
 
-        def quantise_products(pair):
-            codes[pair] = work.tile([P, 2, 2, P], U32, tag="codes", name="codes", align_bytes=64)
-            scales[pair] = work.tile([P, 2, 2, P], U8, tag="scales", name="scales", align_bytes=64)
+        def quantise_products(pair, halves):
+            if halves.start == 0:
+                codes[pair] = work.tile([P, 2, 2, P], U32, tag="codes", name="codes", align_bytes=64)
+                scales[pair] = work.tile([P, 2, 2, P], U8, tag="scales", name="scales", align_bytes=64)
             nc.vector.quantize_mx(
-                out=codes[pair][:].rearrange("p h a r -> p (h a r)").bitcast(FP8X4),
-                scales=scales[pair][:].rearrange("p h a r -> p (h a r)"),
-                in_=grouped[pair][:].rearrange("p h a r t -> p (h a r t)"),
+                out=codes[pair][:, halves].rearrange("p h a r -> p (h a r)").bitcast(FP8X4),
+                scales=scales[pair][:, halves].rearrange("p h a r -> p (h a r)"),
+                in_=grouped[pair][:, halves].rearrange("p h a r t -> p (h a r t)"),
             )
 
         def logits(n):
@@ -273,7 +277,7 @@ def tile_vnclcell_pb_e_kernel(
                 nc.scalar.activation(out=squashed[:, j, :], in_=new_cell[:, j, :], func=ACT.Tanh)
                 value = work.tile([P, WIDTH], F32, tag="value", name="value")
                 nc.scalar.activation(out=value[:], in_=total[n][:], func=ACT.Sigmoid)
-                hidden = work.tile([P, WIDTH], F32, tag="hidden", name="hidden")
+                hidden = work.tile([P, WIDTH], F32, tag="hidden", name="hidden", bufs=ROW_TILES)
                 nc.vector.tensor_tensor(out=hidden[:], in0=value[:], in1=squashed[:, j, :], op=ALU.mult)
                 nc.sync.dma_start(out=by_row_tile(out_0)[:, j, :], in_=hidden[:])
 
@@ -288,9 +292,13 @@ def tile_vnclcell_pb_e_kernel(
                 add_bias_tensor(n - 2)
             if 1 <= n <= UNITS:
                 flip_products(n - 1)
+            if 2 <= n < UNITS and n % 2 == 0:
+                quantise_products(n // 2 - 1, slice(0, 2))
+            if n == UNITS - 1:
+                quantise_products(n // 2, slice(0, 1))
+            if n == UNITS:
+                quantise_products(n // 2 - 1, slice(1, 2))
             if 3 <= n <= UNITS + 2:
                 logits(n - 3)
-            if 2 <= n <= UNITS and n % 2 == 0:
-                quantise_products(n // 2 - 1)
             if n >= 4:
                 gate(n - 4)

@@ -100,14 +100,12 @@ def tile_vnclcell_pb_e_kernel(
             out=bias_row[0:1].rearrange("p g c -> p (g c)"),
             in_=b.rearrange("g c -> (g c)").unsqueeze(0),
         )
+        load_rows(nc.gpsimd, "h")
+        nc.gpsimd.dma_start(out=visual[:, GATE_ORDER[0]], in_=by_row_tile(logits_v[GATE_ORDER[0]]))
+        nc.gpsimd.dma_start(out=cell[:], in_=by_row_tile(rnn_c))
         for name in WEIGHTS:
-            if name == "Ua":
-                load_rows(nc.sync, "h")
-            if name == "Wc":
-                nc.sync.dma_start(out=visual[:, GATE_ORDER[0]], in_=by_row_tile(logits_v[GATE_ORDER[0]]))
             load_plane(name)
             load_words(name, GATE_ORDER[0])
-        nc.sync.dma_start(out=cell[:], in_=by_row_tile(rnn_c))
         for e in GATE_ORDER[1:]:
             for name in WEIGHTS:
                 load_words(name, e)

@@ -47,9 +47,8 @@ def tile_vnclcell_pb_e_kernel(
         ctx.enter_context(tc.manual_schedule())
         keep = ctx.enter_context(tc.tile_pool(name="keep", bufs=1))
         work = ctx.enter_context(tc.tile_pool(name="work", bufs=3))
-        first_psum = ctx.enter_context(tc.psum_pool(name="first_psum", bufs=4))
+        first_psum = ctx.enter_context(tc.psum_pool(name="first_psum", bufs=5))
         flip_psum = ctx.enter_context(tc.psum_pool(name="flip_psum", bufs=1))
-        addend_psum = ctx.enter_context(tc.psum_pool(name="addend_psum", bufs=1))
         logit_psum = ctx.enter_context(tc.psum_pool(name="logit_psum", bufs=2))
 
         planes = keep.tile([P, len(WEIGHTS), WIDTH], U8, align_bytes=64)
@@ -101,15 +100,16 @@ def tile_vnclcell_pb_e_kernel(
             in_=b.rearrange("g c -> (g c)").unsqueeze(0),
         )
         load_rows(nc.gpsimd, "h")
-        nc.gpsimd.dma_start(out=visual[:, GATE_ORDER[0]], in_=by_row_tile(logits_v[GATE_ORDER[0]]))
         nc.gpsimd.dma_start(out=cell[:], in_=by_row_tile(rnn_c))
         for name in WEIGHTS:
+            if name == "Wc":
+                nc.sync.dma_start(out=visual[:, GATE_ORDER[0]], in_=by_row_tile(logits_v[GATE_ORDER[0]]))
             load_plane(name)
             load_words(name, GATE_ORDER[0])
         for e in GATE_ORDER[1:]:
+            nc.sync.dma_start(out=visual[:, e], in_=by_row_tile(logits_v[e]))
             for name in WEIGHTS:
                 load_words(name, e)
-            nc.sync.dma_start(out=visual[:, e], in_=by_row_tile(logits_v[e]))
 
         row_codes = {}
         row_scales = {}
@@ -190,19 +190,16 @@ def tile_vnclcell_pb_e_kernel(
 
         def add_bias_gpsimd(n):
             e, j = GATE_ORDER[n // ROW_TILES], n % ROW_TILES
-            addend[n] = work.tile([P, WIDTH], F32, tag="addend_gpsimd", name="addend", bufs=ROW_TILES)
+            addend[n] = work.tile([P, WIDTH], F32, tag="addend_gpsimd", name="addend", bufs=2 * ROW_TILES)
             nc.gpsimd.tensor_tensor(out=addend[n][:], in0=visual[:, e, j, :], in1=bias[:, e, :], op=ALU.add)
 
         def add_bias_tensor(n):
             e, j = GATE_ORDER[n // ROW_TILES], n % ROW_TILES
-            summed = addend_psum.tile([P, WIDTH], F32, tag="summed", name="summed")
+            summed = logit_psum.tile([P, WIDTH], F32, tag="logit", name="summed")
             nc.tensor.matmul(out=summed[:], lhsT=ident_bf16[:], rhs=visual[:, e, j, :], start=True, stop=False)
             nc.tensor.matmul(out=summed[:], lhsT=first_row_ones[:], rhs=bias_row[:, e, :], start=False, stop=True)
             addend[n] = work.tile([P, WIDTH], F32, tag="addend_tensor", name="addend", bufs=2)
-            if n % 4 == 1:
-                nc.vector.tensor_copy(out=addend[n][:], in_=summed[:])
-            else:
-                nc.scalar.copy(out=addend[n][:], in_=summed[:])
+            nc.scalar.copy(out=addend[n][:], in_=summed[:])
 
         def products(n):
             e, j = GATE_ORDER[n // ROW_TILES], n % ROW_TILES
@@ -226,10 +223,7 @@ def tile_vnclcell_pb_e_kernel(
             target = grouped[pair][:, half].rearrange("p a r t -> p a (r t)").bitcast(F32)
             target = target.rearrange("p a (r u) -> p a r u", u=2)
             source = flipped[:].rearrange("p a u r -> p a r u")
-            if n % 4 == 0:
-                nc.vector.tensor_copy(out=target, in_=source)
-            else:
-                nc.scalar.copy(out=target, in_=source)
+            nc.scalar.copy(out=target, in_=source)
 
         def quantise_products(pair, halves):
             if halves.start == 0:
@@ -279,15 +273,11 @@ def tile_vnclcell_pb_e_kernel(
                 nc.vector.tensor_tensor(out=hidden[:], in0=value[:], in1=squashed[:, j, :], op=ALU.mult)
                 nc.sync.dma_start(out=by_row_tile(out_0)[:, j, :], in_=hidden[:])
 
-        for n in range(0, ROW_TILES, 2):
-            add_bias_gpsimd(n)
         for n in range(UNITS + 4):
-            if n + ROW_TILES < UNITS and n % 2 == 0:
-                add_bias_gpsimd(n + ROW_TILES)
             if n < UNITS:
                 products(n)
-            if 3 <= n <= UNITS + 1 and n % 2 == 1:
-                add_bias_tensor(n - 2)
+            if n < UNITS and GATE_ORDER[n // ROW_TILES] != GATE_O:
+                add_bias_gpsimd(n)
             if 1 <= n <= UNITS:
                 flip_products(n - 1)
             if 2 <= n < UNITS and n % 2 == 0:
@@ -296,6 +286,8 @@ def tile_vnclcell_pb_e_kernel(
                 quantise_products(n // 2, slice(0, 1))
             if n == UNITS:
                 quantise_products(n // 2 - 1, slice(1, 2))
+            if 2 <= n < UNITS + 2 and GATE_ORDER[(n - 2) // ROW_TILES] == GATE_O:
+                add_bias_tensor(n - 2)
             if 3 <= n <= UNITS + 2:
                 logits(n - 3)
             if n >= 4:

@@ -24,6 +24,8 @@ UNITS = len(GATE_ORDER) * ROW_TILES
 
 WEIGHTS = ("Wb", "Wa", "Ua", "Ub", "Wc", "Uc")
 
+ADDEND_MAKER = (("gpsimd", "gpsimd"), ("gpsimd", "gpsimd"), ("gpsimd", "gpsimd"), ("tensor", "tensor"))
+
 FLOPS = 2 * 6 * 4 * WIDTH * WIDTH * WIDTH
 
 
@@ -52,15 +54,18 @@ def tile_vnclcell_pb_e_kernel(
         logit_psum = ctx.enter_context(tc.psum_pool(name="logit_psum", bufs=2))
 
         planes = keep.tile([P, len(WEIGHTS), WIDTH], U8, align_bytes=64)
-        nc.vector.memset(planes[:].bitcast(I32), 0)
-        bias_row = keep.tile([P, len(GATE_ORDER), WIDTH], BF16)
-        nc.vector.memset(bias_row[:], 0.0)
-        first_row_ones = keep.tile([P, P], BF16)
-        nc.vector.memset(first_row_ones[:], 0.0)
-        nc.vector.memset(first_row_ones[0:1, :], 1.0)
         warm_in = keep.tile([P, 1], F32)
         warm_out = keep.tile([P, 1], F32)
         nc.vector.memset(warm_in[:], 0.0)
+        idle = keep.tile([P, WIDTH], BF16)
+        nc.vector.memset(idle[:].bitcast(I32), 0)
+        for index in range(len(WEIGHTS)):
+            nc.vector.memset(planes[:, index, :].bitcast(I32), 0)
+        bias_row = keep.tile([P, len(GATE_ORDER), WIDTH], BF16)
+        nc.vector.memset(bias_row[:].rearrange("p g c -> p (g c)").bitcast(I32), 0)
+        first_row_ones = keep.tile([P, P], BF16)
+        nc.vector.memset(first_row_ones[:], 0.0)
+        nc.vector.memset(first_row_ones[0:1, :], 1.0)
         ident_f32 = keep.tile([P, P], F32)
         make_identity(nc, ident_f32[:])
         ident_bf16 = keep.tile([P, P], BF16)
@@ -100,64 +105,67 @@ def tile_vnclcell_pb_e_kernel(
             in_=b.rearrange("g c -> (g c)").unsqueeze(0),
         )
         load_rows(nc.gpsimd, "h")
-        nc.gpsimd.dma_start(out=cell[:], in_=by_row_tile(rnn_c))
+        nc.gpsimd.dma_start(out=visual[:, GATE_ORDER[0]], in_=by_row_tile(logits_v[GATE_ORDER[0]]))
         for name in WEIGHTS:
-            if name == "Wc":
-                nc.sync.dma_start(out=visual[:, GATE_ORDER[0]], in_=by_row_tile(logits_v[GATE_ORDER[0]]))
             load_plane(name)
             load_words(name, GATE_ORDER[0])
+        nc.sync.dma_start(out=cell[:], in_=by_row_tile(rnn_c))
         for e in GATE_ORDER[1:]:
-            nc.sync.dma_start(out=visual[:, e], in_=by_row_tile(logits_v[e]))
             for name in WEIGHTS:
                 load_words(name, e)
+            nc.sync.dma_start(out=visual[:, e], in_=by_row_tile(logits_v[e]))
 
         row_codes = {}
         row_scales = {}
         row_grouped = {}
-
-        def flip_rows(name):
+        for name in ("s", "x", "h"):
             row_grouped[name] = keep.tile([P, ROW_TILES, WIDTH], BF16, name="grouped_" + name, align_bytes=64)
-            for half in range(2):
-                flipped = first_psum.tile([P, 2, 2, P], F32, tag="first", name="flipped_" + name)
-                for jj in range(2):
-                    pairs = raw[name][:, 2 * half + jj, :].bitcast(F32)
-                    for u in range(2):
-                        nc.tensor.transpose(flipped[:, jj, u, :], pairs[:, u : WIDTH // 2 : 2], ident_f32[:])
-                target = row_grouped[name][:, 2 * half : 2 * half + 2, :].bitcast(F32)
-                target = target.rearrange("p jj (r u) -> p jj r u", u=2)
-                source = flipped[:].rearrange("p jj u r -> p jj r u")
-                if half == 0:
-                    nc.vector.tensor_copy(out=target, in_=source)
-                else:
-                    nc.scalar.copy(out=target, in_=source)
-
-        def quantise_rows(name):
             row_codes[name] = keep.tile([P, ROW_TILES * P], U32, name="codes_" + name, align_bytes=64)
             row_scales[name] = keep.tile([P, ROW_TILES * P], U8, name="scales_" + name, align_bytes=64)
+
+        COPIES = (nc.vector.tensor_copy, nc.scalar.copy)
+
+        def flip_rows(name, half, copy):
+            flipped = first_psum.tile([P, 2, 2, P], F32, tag="first", name="flipped_" + name)
+            for jj in range(2):
+                pairs = raw[name][:, 2 * half + jj, :].bitcast(F32)
+                for u in range(2):
+                    nc.tensor.transpose(flipped[:, jj, u, :], pairs[:, u : WIDTH // 2 : 2], ident_f32[:])
+            target = row_grouped[name][:, 2 * half : 2 * half + 2, :].bitcast(F32)
+            target = target.rearrange("p jj (r u) -> p jj r u", u=2)
+            source = flipped[:].rearrange("p jj u r -> p jj r u")
+            copy(out=target, in_=source)
+
+        def quantise_rows(name, tiles):
+            cols = slice(tiles.start * P, tiles.stop * P)
             nc.vector.quantize_mx(
-                out=row_codes[name][:].bitcast(FP8X4),
-                scales=row_scales[name][:],
-                in_=row_grouped[name][:].rearrange("p j c -> p (j c)"),
+                out=row_codes[name][:, cols].bitcast(FP8X4),
+                scales=row_scales[name][:, cols],
+                in_=row_grouped[name][:, tiles].rearrange("p j c -> p (j c)"),
             )
 
-        def spread_bias(e):
-            spread = first_psum.tile([P, WIDTH], F32, tag="first", name="spread")
-            nc.tensor.matmul(out=spread[:], lhsT=first_row_ones[:], rhs=bias_row[:, e, :], start=True, stop=True)
-            if e % 2 == 0:
-                nc.vector.tensor_copy(out=bias[:, e, :], in_=spread[:])
-            else:
-                nc.scalar.copy(out=bias[:, e, :], in_=spread[:])
+        def spread_bias(e, copy):
+            spread = logit_psum.tile([P, 2, WIDTH], BF16, tag="logit", name="spread")
+            for i in range(2):
+                nc.tensor.matmul(
+                    out=spread[:, i], lhsT=first_row_ones[:], rhs=bias_row[:, e + i, :], start=True, stop=True
+                )
+            copy(out=bias[:, e : e + 2, :], in_=spread[:])
 
-        flip_rows("s")
-        flip_rows("x")
-        quantise_rows("s")
-        spread_bias(0)
-        spread_bias(1)
-        quantise_rows("x")
-        spread_bias(2)
-        spread_bias(3)
-        flip_rows("h")
-        quantise_rows("h")
+        for warm in range(4):
+            sink = first_psum.tile([P, WIDTH], F32, tag="first", name="sink")
+            nc.tensor.matmul(out=sink[:], lhsT=idle[:, :P], rhs=idle[:], start=True, stop=True)
+
+        for name in ("s", "x"):
+            flip_rows(name, 0, COPIES[0])
+            flip_rows(name, 1, COPIES[1])
+        for name in ("s", "x"):
+            quantise_rows(name, slice(0, ROW_TILES))
+        flip_rows("h", 0, COPIES[0])
+        flip_rows("h", 1, COPIES[1])
+        spread_bias(0, nc.vector.tensor_copy)
+        quantise_rows("h", slice(0, ROW_TILES))
+        spread_bias(2, nc.vector.tensor_copy)
 
         forget_cell = keep.tile([P, ROW_TILES, WIDTH], F32)
         input_gate = keep.tile([P, ROW_TILES, WIDTH], F32)
@@ -165,6 +173,8 @@ def tile_vnclcell_pb_e_kernel(
         squashed = keep.tile([P, ROW_TILES, WIDTH], F32)
         total = {}
         addend = {}
+        logit = {}
+        fresh = {}
         product = {}
         grouped = {}
         codes = {}
@@ -188,18 +198,19 @@ def tile_vnclcell_pb_e_kernel(
             )
             return acc[:].rearrange("p (c u e) -> p u c e", u=2, e=2)
 
-        def add_bias_gpsimd(n):
+        def add_bias(n):
             e, j = GATE_ORDER[n // ROW_TILES], n % ROW_TILES
-            addend[n] = work.tile([P, WIDTH], F32, tag="addend_gpsimd", name="addend", bufs=2 * ROW_TILES)
-            nc.gpsimd.tensor_tensor(out=addend[n][:], in0=visual[:, e, j, :], in1=bias[:, e, :], op=ALU.add)
-
-        def add_bias_tensor(n):
-            e, j = GATE_ORDER[n // ROW_TILES], n % ROW_TILES
-            summed = logit_psum.tile([P, WIDTH], F32, tag="logit", name="summed")
-            nc.tensor.matmul(out=summed[:], lhsT=ident_bf16[:], rhs=visual[:, e, j, :], start=True, stop=False)
-            nc.tensor.matmul(out=summed[:], lhsT=first_row_ones[:], rhs=bias_row[:, e, :], start=False, stop=True)
-            addend[n] = work.tile([P, WIDTH], F32, tag="addend_tensor", name="addend", bufs=2)
-            nc.scalar.copy(out=addend[n][:], in_=summed[:])
+            addend[n] = work.tile([P, WIDTH], F32, tag="addend", name="addend", bufs=3 * ROW_TILES)
+            maker = ADDEND_MAKER[n // ROW_TILES][j % 2]
+            if maker == "gpsimd":
+                nc.gpsimd.tensor_tensor(out=addend[n][:], in0=visual[:, e, j, :], in1=bias[:, e, :], op=ALU.add)
+            elif maker == "vector":
+                nc.vector.tensor_tensor(out=addend[n][:], in0=visual[:, e, j, :], in1=bias[:, e, :], op=ALU.add)
+            else:
+                summed = first_psum.tile([P, WIDTH], F32, tag="first", name="summed")
+                nc.tensor.matmul(out=summed[:], lhsT=ident_bf16[:], rhs=visual[:, e, j, :], start=True, stop=False)
+                nc.tensor.matmul(out=summed[:], lhsT=first_row_ones[:], rhs=bias_row[:, e, :], start=False, stop=True)
+                nc.scalar.copy(out=addend[n][:], in_=summed[:])
 
         def products(n):
             e, j = GATE_ORDER[n // ROW_TILES], n % ROW_TILES
@@ -237,58 +248,83 @@ def tile_vnclcell_pb_e_kernel(
 
         def logits(n):
             e, j = GATE_ORDER[n // ROW_TILES], n % ROW_TILES
-            logit = logit_psum.tile([P, WIDTH], F32, tag="logit", name="logit")
+            logit[n] = logit_psum.tile([P, WIDTH], F32, tag="logit", name="logit")
             for branch, name in enumerate(("Wc", "Uc")):
                 nc.tensor.matmul_mx(
-                    out=logit[:],
+                    out=logit[n][:],
                     lhsT=codes[n // 2][:, n % 2, branch, :].bitcast(FP8X4),
                     lhsT_scale=scales[n // 2][:, n % 2, branch, :],
                     start=(branch == 0),
                     stop=(branch == 1),
                     **weight_operand(name, e),
                 )
+
+        def columns(n):
+            parts = 2 if n >= UNITS - 2 else 1
+            return [slice(i * WIDTH // parts, (i + 1) * WIDTH // parts) for i in range(parts)]
+
+        def add(n):
             total[n] = work.tile([P, WIDTH], F32, tag="total", name="total")
-            nc.vector.tensor_tensor(out=total[n][:], in0=logit[:], in1=addend[n][:], op=ALU.add)
+            for cols in columns(n):
+                nc.vector.tensor_tensor(
+                    out=total[n][:, cols], in0=logit[n][:, cols], in1=addend[n][:, cols], op=ALU.add
+                )
 
         def gate(n):
             e, j = GATE_ORDER[n // ROW_TILES], n % ROW_TILES
             if e == GATE_F:
-                value = work.tile([P, WIDTH], F32, tag="value", name="value")
+                value = work.tile([P, WIDTH], F32, tag="value", name="value", bufs=ROW_TILES)
                 nc.scalar.activation(out=value[:], in_=total[n][:], func=ACT.Sigmoid)
                 nc.gpsimd.tensor_tensor(out=forget_cell[:, j, :], in0=value[:], in1=cell[:, j, :], op=ALU.mult)
             elif e == GATE_I:
                 nc.scalar.activation(out=input_gate[:, j, :], in_=total[n][:], func=ACT.Sigmoid)
             elif e == GATE_G:
-                value = work.tile([P, WIDTH], F32, tag="value", name="value")
+                value = work.tile([P, WIDTH], F32, tag="value", name="value", bufs=ROW_TILES)
                 nc.scalar.activation(out=value[:], in_=total[n][:], func=ACT.Tanh)
-                fresh = work.tile([P, WIDTH], F32, tag="fresh", name="fresh")
-                nc.gpsimd.tensor_tensor(out=fresh[:], in0=value[:], in1=input_gate[:, j, :], op=ALU.mult)
-                nc.gpsimd.tensor_tensor(out=new_cell[:, j, :], in0=fresh[:], in1=forget_cell[:, j, :], op=ALU.add)
-                nc.sync.dma_start(out=by_row_tile(out_1)[:, j, :], in_=new_cell[:, j, :])
+                fresh[j] = work.tile([P, WIDTH], F32, tag="fresh", name="fresh", bufs=ROW_TILES)
+                nc.gpsimd.tensor_tensor(out=fresh[j][:], in0=value[:], in1=input_gate[:, j, :], op=ALU.mult)
             else:
-                nc.scalar.activation(out=squashed[:, j, :], in_=new_cell[:, j, :], func=ACT.Tanh)
-                value = work.tile([P, WIDTH], F32, tag="value", name="value")
-                nc.scalar.activation(out=value[:], in_=total[n][:], func=ACT.Sigmoid)
+                value = work.tile([P, WIDTH], F32, tag="value", name="value", bufs=ROW_TILES)
                 hidden = work.tile([P, WIDTH], F32, tag="hidden", name="hidden", bufs=ROW_TILES)
-                nc.vector.tensor_tensor(out=hidden[:], in0=value[:], in1=squashed[:, j, :], op=ALU.mult)
-                nc.sync.dma_start(out=by_row_tile(out_0)[:, j, :], in_=hidden[:])
+                for cols in columns(n):
+                    nc.scalar.activation(out=value[:, cols], in_=total[n][:, cols], func=ACT.Sigmoid)
+                    nc.vector.tensor_tensor(
+                        out=hidden[:, cols], in0=value[:, cols], in1=squashed[:, j, cols], op=ALU.mult
+                    )
+                    nc.sync.dma_start(out=by_row_tile(out_0)[:, j, cols], in_=hidden[:, cols])
+
+        def close_cell(j):
+            nc.vector.tensor_tensor(out=new_cell[:, j, :], in0=fresh[j][:], in1=forget_cell[:, j, :], op=ALU.add)
+            nc.sync.dma_start(out=by_row_tile(out_1)[:, j, :], in_=new_cell[:, j, :])
+
+        def squash_cell(j):
+            nc.scalar.activation(out=squashed[:, j, :], in_=new_cell[:, j, :], func=ACT.Tanh)
+
+        def maker(n):
+            return ADDEND_MAKER[n // ROW_TILES][n % 2]
 
         for n in range(UNITS + 4):
             if n < UNITS:
                 products(n)
-            if n < UNITS and GATE_ORDER[n // ROW_TILES] != GATE_O:
-                add_bias_gpsimd(n)
+            if 2 <= n < UNITS + 2 and maker(n - 2) == "tensor":
+                add_bias(n - 2)
+            for ahead in range(4) if n == 0 else range(n + 3, n + 4):
+                if ahead < UNITS and maker(ahead) == "gpsimd":
+                    add_bias(ahead)
             if 1 <= n <= UNITS:
                 flip_products(n - 1)
+            if 13 <= n < 13 + ROW_TILES:
+                close_cell(n - 13)
             if 2 <= n < UNITS and n % 2 == 0:
                 quantise_products(n // 2 - 1, slice(0, 2))
             if n == UNITS - 1:
                 quantise_products(n // 2, slice(0, 1))
             if n == UNITS:
                 quantise_products(n // 2 - 1, slice(1, 2))
-            if 2 <= n < UNITS + 2 and GATE_ORDER[(n - 2) // ROW_TILES] == GATE_O:
-                add_bias_tensor(n - 2)
-            if 3 <= n <= UNITS + 2:
+            if 3 <= n < UNITS + 3:
                 logits(n - 3)
+                add(n - 3)
             if n >= 4:
                 gate(n - 4)
+            if 15 <= n < 15 + ROW_TILES:
+                squash_cell(n - 15)

@@ -91,6 +91,12 @@ def tile_vnclcell_pb_e_kernel(
                     in_=scales_dram[name][:, 4 * quadrant : 4 * quadrant + 4, :].bitcast(I32),
                 )
 
+        def load_first_words(name):
+            nc.gpsimd.dma_start(
+                out=words[name][:, GATE_ORDER[0], :].bitcast(F32),
+                in_=words_dram[name][GATE_ORDER[0]].rearrange("p n t -> p (n t)").bitcast(F32),
+            )
+
         def load_words(name, e):
             nc.sync.dma_start(
                 out=words[name][:, e, :].bitcast(I32),
@@ -105,15 +111,32 @@ def tile_vnclcell_pb_e_kernel(
             in_=b.rearrange("g c -> (g c)").unsqueeze(0),
         )
         load_rows(nc.gpsimd, "h")
-        nc.gpsimd.dma_start(out=visual[:, GATE_ORDER[0]], in_=by_row_tile(logits_v[GATE_ORDER[0]]))
+        load_first_words("Ua")
+        load_first_words("Ub")
+        load_plane("Wb")
+        load_words("Wb", GATE_ORDER[0])
+        load_plane("Wa")
+        load_words("Wa", GATE_ORDER[0])
+        load_plane("Ua")
+        load_plane("Ub")
+        nc.sync.dma_start(out=visual[:, GATE_ORDER[0]], in_=by_row_tile(logits_v[GATE_ORDER[0]]))
+        load_plane("Wc")
+        load_words("Wc", GATE_ORDER[0])
+        load_plane("Uc")
+        load_words("Uc", GATE_ORDER[0])
         for name in WEIGHTS:
-            load_plane(name)
-            load_words(name, GATE_ORDER[0])
+            load_words(name, GATE_ORDER[1])
         nc.sync.dma_start(out=cell[:], in_=by_row_tile(rnn_c))
-        for e in GATE_ORDER[1:]:
-            for name in WEIGHTS:
-                load_words(name, e)
-            nc.sync.dma_start(out=visual[:, e], in_=by_row_tile(logits_v[e]))
+        nc.sync.dma_start(out=visual[:, GATE_ORDER[1]], in_=by_row_tile(logits_v[GATE_ORDER[1]]))
+        for name in WEIGHTS:
+            nc.sync.dma_start(
+                out=words[name][:, 2:4, :].bitcast(I32),
+                in_=words_dram[name][2:4].rearrange("e p n t -> p e (n t)").bitcast(I32),
+            )
+        nc.sync.dma_start(
+            out=visual[:, 2:4].rearrange("p e j c -> p e (j c)"),
+            in_=logits_v[2:4].rearrange("e (p j) c -> p e (j c)", j=ROW_TILES),
+        )
 
         row_codes = {}
         row_scales = {}
@@ -144,28 +167,42 @@ def tile_vnclcell_pb_e_kernel(
                 in_=row_grouped[name][:, tiles].rearrange("p j c -> p (j c)"),
             )
 
-        def spread_bias(e, copy):
+        spreads = {}
+
+        def spread_bias(e):
             spread = logit_psum.tile([P, 2, WIDTH], BF16, tag="logit", name="spread")
             for i in range(2):
                 nc.tensor.matmul(
                     out=spread[:, i], lhsT=first_row_ones[:], rhs=bias_row[:, e + i, :], start=True, stop=True
                 )
-            copy(out=bias[:, e : e + 2, :], in_=spread[:])
+            spreads[e] = spread
 
-        for warm in range(4):
+        def keep_bias(e, copy):
+            copy(out=bias[:, e : e + 2, :], in_=spreads[e][:])
+
+        for warm in range(6):
             sink = first_psum.tile([P, WIDTH], F32, tag="first", name="sink")
             nc.tensor.matmul(out=sink[:], lhsT=idle[:, :P], rhs=idle[:], start=True, stop=True)
 
-        for name in ("s", "x"):
-            flip_rows(name, 0, COPIES[0])
-            flip_rows(name, 1, COPIES[1])
-        for name in ("s", "x"):
-            quantise_rows(name, slice(0, ROW_TILES))
+        flip_rows("s", 0, COPIES[0])
+        flip_rows("s", 1, COPIES[1])
+        for extra in range(2):
+            sink = first_psum.tile([P, WIDTH], F32, tag="first", name="sink")
+            nc.tensor.matmul(out=sink[:], lhsT=idle[:, :P], rhs=idle[:], start=True, stop=True)
+        flip_rows("x", 0, COPIES[0])
+        flip_rows("x", 1, COPIES[1])
+        for extra in range(2):
+            sink = first_psum.tile([P, WIDTH], F32, tag="first", name="sink")
+            nc.tensor.matmul(out=sink[:], lhsT=idle[:, :P], rhs=idle[:], start=True, stop=True)
+        quantise_rows("s", slice(0, ROW_TILES))
+        quantise_rows("x", slice(0, ROW_TILES))
         flip_rows("h", 0, COPIES[0])
         flip_rows("h", 1, COPIES[1])
-        spread_bias(0, nc.vector.tensor_copy)
+        spread_bias(0)
+        keep_bias(0, nc.vector.tensor_copy)
         quantise_rows("h", slice(0, ROW_TILES))
-        spread_bias(2, nc.vector.tensor_copy)
+        spread_bias(2)
+        keep_bias(2, nc.vector.tensor_copy)
 
         forget_cell = keep.tile([P, ROW_TILES, WIDTH], F32)
         input_gate = keep.tile([P, ROW_TILES, WIDTH], F32)
@@ -295,7 +332,8 @@ def tile_vnclcell_pb_e_kernel(
 
         def close_cell(j):
             nc.vector.tensor_tensor(out=new_cell[:, j, :], in0=fresh[j][:], in1=forget_cell[:, j, :], op=ALU.add)
-            nc.sync.dma_start(out=by_row_tile(out_1)[:, j, :], in_=new_cell[:, j, :])
+            if j % 2 == 1:
+                nc.sync.dma_start(out=by_row_tile(out_1)[:, j - 1 : j + 1, :], in_=new_cell[:, j - 1 : j + 1, :])
 
         def squash_cell(j):
             nc.scalar.activation(out=squashed[:, j, :], in_=new_cell[:, j, :], func=ACT.Tanh)
@@ -313,8 +351,8 @@ def tile_vnclcell_pb_e_kernel(
                     add_bias(ahead)
             if 1 <= n <= UNITS:
                 flip_products(n - 1)
-            if 13 <= n < 13 + ROW_TILES:
-                close_cell(n - 13)
+            if 14 <= n < 14 + ROW_TILES:
+                close_cell(n - 14)
             if 2 <= n < UNITS and n % 2 == 0:
                 quantise_products(n // 2 - 1, slice(0, 2))
             if n == UNITS - 1:

@@ -110,13 +110,13 @@ def tile_vnclcell_pb_e_kernel(
             out=bias_row[0:1].rearrange("p g c -> p (g c)"),
             in_=b.rearrange("g c -> (g c)").unsqueeze(0),
         )
+        load_first_words("Wa")
         load_rows(nc.gpsimd, "h")
         load_first_words("Ua")
         load_first_words("Ub")
         load_plane("Wb")
         load_words("Wb", GATE_ORDER[0])
         load_plane("Wa")
-        load_words("Wa", GATE_ORDER[0])
         load_plane("Ua")
         load_plane("Ub")
         nc.sync.dma_start(out=visual[:, GATE_ORDER[0]], in_=by_row_tile(logits_v[GATE_ORDER[0]]))
@@ -133,10 +133,8 @@ def tile_vnclcell_pb_e_kernel(
                 out=words[name][:, 2:4, :].bitcast(I32),
                 in_=words_dram[name][2:4].rearrange("e p n t -> p e (n t)").bitcast(I32),
             )
-        nc.sync.dma_start(
-            out=visual[:, 2:4].rearrange("p e j c -> p e (j c)"),
-            in_=logits_v[2:4].rearrange("e (p j) c -> p e (j c)", j=ROW_TILES),
-        )
+        for e in GATE_ORDER[2:]:
+            nc.sync.dma_start(out=visual[:, e], in_=by_row_tile(logits_v[e]))
 
         row_codes = {}
         row_scales = {}
@@ -186,22 +184,16 @@ def tile_vnclcell_pb_e_kernel(
 
         flip_rows("s", 0, COPIES[0])
         flip_rows("s", 1, COPIES[1])
-        for extra in range(2):
-            sink = first_psum.tile([P, WIDTH], F32, tag="first", name="sink")
-            nc.tensor.matmul(out=sink[:], lhsT=idle[:, :P], rhs=idle[:], start=True, stop=True)
+        spread_bias(0)
         flip_rows("x", 0, COPIES[0])
         flip_rows("x", 1, COPIES[1])
-        for extra in range(2):
-            sink = first_psum.tile([P, WIDTH], F32, tag="first", name="sink")
-            nc.tensor.matmul(out=sink[:], lhsT=idle[:, :P], rhs=idle[:], start=True, stop=True)
+        spread_bias(2)
         quantise_rows("s", slice(0, ROW_TILES))
         quantise_rows("x", slice(0, ROW_TILES))
         flip_rows("h", 0, COPIES[0])
         flip_rows("h", 1, COPIES[1])
-        spread_bias(0)
         keep_bias(0, nc.vector.tensor_copy)
         quantise_rows("h", slice(0, ROW_TILES))
-        spread_bias(2)
         keep_bias(2, nc.vector.tensor_copy)
 
         forget_cell = keep.tile([P, ROW_TILES, WIDTH], F32)

from contextlib import ExitStack

import concourse.mybir as mybir
from concourse.masks import make_identity

FP8X4 = mybir.dt.float8_e4m3fn_x4
BF16 = mybir.dt.bfloat16
F32 = mybir.dt.float32
I32 = mybir.dt.int32
U32 = mybir.dt.uint32
U8 = mybir.dt.uint8
ACT = mybir.ActivationFunctionType
ALU = mybir.AluOpType

P = 128
PACK = 4
WIDTH = 512
ROW_TILES = 4
QUADRANTS = 4

GATE_I, GATE_F, GATE_O, GATE_G = 0, 1, 2, 3
GATE_ORDER = (GATE_F, GATE_I, GATE_G, GATE_O)
UNITS = len(GATE_ORDER) * ROW_TILES

WEIGHTS = ("Wb", "Wa", "Ua", "Ub", "Wc", "Uc")

ADDEND_MAKER = (("gpsimd", "gpsimd"), ("gpsimd", "gpsimd"), ("gpsimd", "gpsimd"), ("tensor", "tensor"))

FLOPS = 2 * 6 * 4 * WIDTH * WIDTH * WIDTH


def tile_vnclcell_pb_e_kernel(
    tc,
    decoder_input, rnn_h, rnn_c, s,
    Wa_words, Wa_scales, Wb_words, Wb_scales, Wc_words, Wc_scales,
    Ua_words, Ua_scales, Ub_words, Ub_scales, Uc_words, Uc_scales,
    logits_v, b,
    out_0, out_1,
):
    nc = tc.nc
    words_dram = {"Wa": Wa_words, "Wb": Wb_words, "Wc": Wc_words, "Ua": Ua_words, "Ub": Ub_words, "Uc": Uc_words}
    scales_dram = {"Wa": Wa_scales, "Wb": Wb_scales, "Wc": Wc_scales, "Ua": Ua_scales, "Ub": Ub_scales, "Uc": Uc_scales}
    rows_dram = {"s": s, "x": decoder_input, "h": rnn_h}

    def by_row_tile(matrix):
        return matrix.rearrange("(p j) c -> p j c", j=ROW_TILES)

    with ExitStack() as ctx:
        ctx.enter_context(tc.manual_schedule())
        keep = ctx.enter_context(tc.tile_pool(name="keep", bufs=1))
        work = ctx.enter_context(tc.tile_pool(name="work", bufs=3))
        first_psum = ctx.enter_context(tc.psum_pool(name="first_psum", bufs=5))
        flip_psum = ctx.enter_context(tc.psum_pool(name="flip_psum", bufs=1))
        logit_psum = ctx.enter_context(tc.psum_pool(name="logit_psum", bufs=2))

        planes = keep.tile([P, len(WEIGHTS), WIDTH], U8, align_bytes=64)
        warm_in = keep.tile([P, 1], F32)
        warm_out = keep.tile([P, 1], F32)
        nc.vector.memset(warm_in[:], 0.0)
        idle = keep.tile([P, WIDTH], BF16)
        nc.vector.memset(idle[:].bitcast(I32), 0)
        for index in range(len(WEIGHTS)):
            nc.vector.memset(planes[:, index, :].bitcast(I32), 0)
        bias_row = keep.tile([P, len(GATE_ORDER), WIDTH], BF16)
        nc.vector.memset(bias_row[:].rearrange("p g c -> p (g c)").bitcast(I32), 0)
        first_row_ones = keep.tile([P, P], BF16)
        nc.vector.memset(first_row_ones[:], 0.0)
        nc.vector.memset(first_row_ones[0:1, :], 1.0)
        ident_f32 = keep.tile([P, P], F32)
        make_identity(nc, ident_f32[:])
        ident_bf16 = keep.tile([P, P], BF16)
        make_identity(nc, ident_bf16[:])

        raw = {}
        for name in ("s", "x", "h"):
            raw[name] = keep.tile([P, ROW_TILES, WIDTH], BF16, name="raw_" + name)
        words = {}
        for name in WEIGHTS:
            words[name] = keep.tile([P, len(GATE_ORDER), WIDTH], U32, name="words_" + name, align_bytes=64)
        visual = keep.tile([P, len(GATE_ORDER), ROW_TILES, WIDTH], BF16)
        bias = keep.tile([P, len(GATE_ORDER), WIDTH], BF16)
        cell = keep.tile([P, ROW_TILES, WIDTH], BF16)

        def load_rows(queue, name):
            queue.dma_start(out=raw[name][:], in_=by_row_tile(rows_dram[name]))

        def load_plane(name):
            for quadrant in range(QUADRANTS):
                nc.sync.dma_start(
                    out=planes[32 * quadrant : 32 * quadrant + 16, WEIGHTS.index(name), :].bitcast(I32),
                    in_=scales_dram[name][:, 4 * quadrant : 4 * quadrant + 4, :].bitcast(I32),
                )

        def load_first_words(name):
            nc.gpsimd.dma_start(
                out=words[name][:, GATE_ORDER[0], :].bitcast(F32),
                in_=words_dram[name][GATE_ORDER[0]].rearrange("p n t -> p (n t)").bitcast(F32),
            )

        def load_words(name, e):
            nc.sync.dma_start(
                out=words[name][:, e, :].bitcast(I32),
                in_=words_dram[name][e].rearrange("p n t -> p (n t)").bitcast(I32),
            )

        load_rows(nc.scalar, "s")
        load_rows(nc.scalar, "x")
        nc.scalar.activation(out=warm_out[:], in_=warm_in[:], func=ACT.Sigmoid)
        nc.scalar.dma_start(
            out=bias_row[0:1].rearrange("p g c -> p (g c)"),
            in_=b.rearrange("g c -> (g c)").unsqueeze(0),
        )
        load_first_words("Wa")
        load_rows(nc.gpsimd, "h")
        load_first_words("Ua")
        load_first_words("Ub")
        load_plane("Wb")
        load_words("Wb", GATE_ORDER[0])
        load_plane("Wa")
        load_plane("Ua")
        load_plane("Ub")
        nc.sync.dma_start(out=visual[:, GATE_ORDER[0]], in_=by_row_tile(logits_v[GATE_ORDER[0]]))
        load_plane("Wc")
        load_words("Wc", GATE_ORDER[0])
        load_plane("Uc")
        load_words("Uc", GATE_ORDER[0])
        for name in WEIGHTS:
            load_words(name, GATE_ORDER[1])
        nc.sync.dma_start(out=cell[:], in_=by_row_tile(rnn_c))
        nc.sync.dma_start(out=visual[:, GATE_ORDER[1]], in_=by_row_tile(logits_v[GATE_ORDER[1]]))
        for name in WEIGHTS:
            nc.sync.dma_start(
                out=words[name][:, 2:4, :].bitcast(I32),
                in_=words_dram[name][2:4].rearrange("e p n t -> p e (n t)").bitcast(I32),
            )
        for e in GATE_ORDER[2:]:
            nc.sync.dma_start(out=visual[:, e], in_=by_row_tile(logits_v[e]))

        row_codes = {}
        row_scales = {}
        row_grouped = {}
        for name in ("s", "x", "h"):
            row_grouped[name] = keep.tile([P, ROW_TILES, WIDTH], BF16, name="grouped_" + name, align_bytes=64)
            row_codes[name] = keep.tile([P, ROW_TILES * P], U32, name="codes_" + name, align_bytes=64)
            row_scales[name] = keep.tile([P, ROW_TILES * P], U8, name="scales_" + name, align_bytes=64)

        COPIES = (nc.vector.tensor_copy, nc.scalar.copy)

        def flip_rows(name, half, copy):
            flipped = first_psum.tile([P, 2, 2, P], F32, tag="first", name="flipped_" + name)
            for jj in range(2):
                pairs = raw[name][:, 2 * half + jj, :].bitcast(F32)
                for u in range(2):
                    nc.tensor.transpose(flipped[:, jj, u, :], pairs[:, u : WIDTH // 2 : 2], ident_f32[:])
            target = row_grouped[name][:, 2 * half : 2 * half + 2, :].bitcast(F32)
            target = target.rearrange("p jj (r u) -> p jj r u", u=2)
            source = flipped[:].rearrange("p jj u r -> p jj r u")
            copy(out=target, in_=source)

        def quantise_rows(name, tiles):
            cols = slice(tiles.start * P, tiles.stop * P)
            nc.vector.quantize_mx(
                out=row_codes[name][:, cols].bitcast(FP8X4),
                scales=row_scales[name][:, cols],
                in_=row_grouped[name][:, tiles].rearrange("p j c -> p (j c)"),
            )

        spreads = {}

        def spread_bias(e):
            spread = logit_psum.tile([P, 2, WIDTH], BF16, tag="logit", name="spread")
            for i in range(2):
                nc.tensor.matmul(
                    out=spread[:, i], lhsT=first_row_ones[:], rhs=bias_row[:, e + i, :], start=True, stop=True
                )
            spreads[e] = spread

        def keep_bias(e, copy):
            copy(out=bias[:, e : e + 2, :], in_=spreads[e][:])

        for warm in range(6):
            sink = first_psum.tile([P, WIDTH], F32, tag="first", name="sink")
            nc.tensor.matmul(out=sink[:], lhsT=idle[:, :P], rhs=idle[:], start=True, stop=True)

        flip_rows("s", 0, COPIES[0])
        flip_rows("s", 1, COPIES[1])
        spread_bias(0)
        flip_rows("x", 0, COPIES[0])
        flip_rows("x", 1, COPIES[1])
        spread_bias(2)
        quantise_rows("s", slice(0, ROW_TILES))
        quantise_rows("x", slice(0, ROW_TILES))
        flip_rows("h", 0, COPIES[0])
        flip_rows("h", 1, COPIES[1])
        keep_bias(0, nc.vector.tensor_copy)
        quantise_rows("h", slice(0, ROW_TILES))
        keep_bias(2, nc.vector.tensor_copy)

        forget_cell = keep.tile([P, ROW_TILES, WIDTH], F32)
        input_gate = keep.tile([P, ROW_TILES, WIDTH], F32)
        new_cell = keep.tile([P, ROW_TILES, WIDTH], F32)
        squashed = keep.tile([P, ROW_TILES, WIDTH], F32)
        total = {}
        addend = {}
        logit = {}
        fresh = {}
        product = {}
        grouped = {}
        codes = {}
        scales = {}

        def weight_operand(name, e):
            return {
                "rhs": words[name][:, e, :].bitcast(FP8X4),
                "rhs_scale": planes[4 * e : P, WEIGHTS.index(name), :],
            }

        def first_matmul(rows, j, name, e):
            acc = first_psum.tile([P, WIDTH], F32, tag="first", name="acc_" + name)
            nc.tensor.matmul_mx(
                out=acc[:],
                lhsT=row_codes[rows][:, j * P : (j + 1) * P].bitcast(FP8X4),
                lhsT_scale=row_scales[rows][:, j * P : (j + 1) * P],
                start=True,
                stop=True,
                **weight_operand(name, e),
            )
            return acc[:].rearrange("p (c u e) -> p u c e", u=2, e=2)

        def add_bias(n):
            e, j = GATE_ORDER[n // ROW_TILES], n % ROW_TILES
            addend[n] = work.tile([P, WIDTH], F32, tag="addend", name="addend", bufs=3 * ROW_TILES)
            maker = ADDEND_MAKER[n // ROW_TILES][j % 2]
            if maker == "gpsimd":
                nc.gpsimd.tensor_tensor(out=addend[n][:], in0=visual[:, e, j, :], in1=bias[:, e, :], op=ALU.add)
            elif maker == "vector":
                nc.vector.tensor_tensor(out=addend[n][:], in0=visual[:, e, j, :], in1=bias[:, e, :], op=ALU.add)
            else:
                summed = first_psum.tile([P, WIDTH], F32, tag="first", name="summed")
                nc.tensor.matmul(out=summed[:], lhsT=ident_bf16[:], rhs=visual[:, e, j, :], start=True, stop=False)
                nc.tensor.matmul(out=summed[:], lhsT=first_row_ones[:], rhs=bias_row[:, e, :], start=False, stop=True)
                nc.scalar.copy(out=addend[n][:], in_=summed[:])

        def products(n):
            e, j = GATE_ORDER[n // ROW_TILES], n % ROW_TILES
            product[n] = work.tile([P, 2, 2, P, 2], BF16, tag="product", name="product")
            for branch, (copied, direct) in enumerate(((("s", "Wb"), ("x", "Wa")), (("h", "Ua"), ("s", "Ub")))):
                copied_acc = first_matmul(copied[0], j, copied[1], e)
                direct_acc = first_matmul(direct[0], j, direct[1], e)
                factor = work.tile([P, 2, P, 2], F32, tag="factor%d" % branch, name="factor")
                nc.scalar.copy(out=factor[:], in_=copied_acc)
                nc.vector.tensor_tensor(out=product[n][:, branch], in0=direct_acc, in1=factor[:], op=ALU.mult)

        def flip_products(n):
            pair, half = n // 2, n % 2
            if half == 0:
                grouped[pair] = work.tile([P, 2, 2, P, PACK], BF16, tag="grouped", name="grouped", align_bytes=64)
            flipped = flip_psum.tile([P, 2, 2, P], F32, tag="flip", name="flipped")
            for branch in range(2):
                for u in range(2):
                    pairs = product[n][:, branch, u].rearrange("p c e -> p (c e)").bitcast(F32)
                    nc.tensor.transpose(flipped[:, branch, u, :], pairs, ident_f32[:])
            target = grouped[pair][:, half].rearrange("p a r t -> p a (r t)").bitcast(F32)
            target = target.rearrange("p a (r u) -> p a r u", u=2)
            source = flipped[:].rearrange("p a u r -> p a r u")
            nc.scalar.copy(out=target, in_=source)

        def quantise_products(pair, halves):
            if halves.start == 0:
                codes[pair] = work.tile([P, 2, 2, P], U32, tag="codes", name="codes", align_bytes=64)
                scales[pair] = work.tile([P, 2, 2, P], U8, tag="scales", name="scales", align_bytes=64)
            nc.vector.quantize_mx(
                out=codes[pair][:, halves].rearrange("p h a r -> p (h a r)").bitcast(FP8X4),
                scales=scales[pair][:, halves].rearrange("p h a r -> p (h a r)"),
                in_=grouped[pair][:, halves].rearrange("p h a r t -> p (h a r t)"),
            )

        def logits(n):
            e, j = GATE_ORDER[n // ROW_TILES], n % ROW_TILES
            logit[n] = logit_psum.tile([P, WIDTH], F32, tag="logit", name="logit")
            for branch, name in enumerate(("Wc", "Uc")):
                nc.tensor.matmul_mx(
                    out=logit[n][:],
                    lhsT=codes[n // 2][:, n % 2, branch, :].bitcast(FP8X4),
                    lhsT_scale=scales[n // 2][:, n % 2, branch, :],
                    start=(branch == 0),
                    stop=(branch == 1),
                    **weight_operand(name, e),
                )

        def columns(n):
            parts = 2 if n >= UNITS - 2 else 1
            return [slice(i * WIDTH // parts, (i + 1) * WIDTH // parts) for i in range(parts)]

        def add(n):
            total[n] = work.tile([P, WIDTH], F32, tag="total", name="total")
            for cols in columns(n):
                nc.vector.tensor_tensor(
                    out=total[n][:, cols], in0=logit[n][:, cols], in1=addend[n][:, cols], op=ALU.add
                )

        def gate(n):
            e, j = GATE_ORDER[n // ROW_TILES], n % ROW_TILES
            if e == GATE_F:
                value = work.tile([P, WIDTH], F32, tag="value", name="value", bufs=ROW_TILES)
                nc.scalar.activation(out=value[:], in_=total[n][:], func=ACT.Sigmoid)
                nc.gpsimd.tensor_tensor(out=forget_cell[:, j, :], in0=value[:], in1=cell[:, j, :], op=ALU.mult)
            elif e == GATE_I:
                nc.scalar.activation(out=input_gate[:, j, :], in_=total[n][:], func=ACT.Sigmoid)
            elif e == GATE_G:
                value = work.tile([P, WIDTH], F32, tag="value", name="value", bufs=ROW_TILES)
                nc.scalar.activation(out=value[:], in_=total[n][:], func=ACT.Tanh)
                fresh[j] = work.tile([P, WIDTH], F32, tag="fresh", name="fresh", bufs=ROW_TILES)
                nc.gpsimd.tensor_tensor(out=fresh[j][:], in0=value[:], in1=input_gate[:, j, :], op=ALU.mult)
            else:
                value = work.tile([P, WIDTH], F32, tag="value", name="value", bufs=ROW_TILES)
                hidden = work.tile([P, WIDTH], F32, tag="hidden", name="hidden", bufs=ROW_TILES)
                for cols in columns(n):
                    nc.scalar.activation(out=value[:, cols], in_=total[n][:, cols], func=ACT.Sigmoid)
                    nc.vector.tensor_tensor(
                        out=hidden[:, cols], in0=value[:, cols], in1=squashed[:, j, cols], op=ALU.mult
                    )
                    nc.sync.dma_start(out=by_row_tile(out_0)[:, j, cols], in_=hidden[:, cols])

        def close_cell(j):
            nc.vector.tensor_tensor(out=new_cell[:, j, :], in0=fresh[j][:], in1=forget_cell[:, j, :], op=ALU.add)
            if j % 2 == 1:
                nc.sync.dma_start(out=by_row_tile(out_1)[:, j - 1 : j + 1, :], in_=new_cell[:, j - 1 : j + 1, :])

        def squash_cell(j):
            nc.scalar.activation(out=squashed[:, j, :], in_=new_cell[:, j, :], func=ACT.Tanh)

        def maker(n):
            return ADDEND_MAKER[n // ROW_TILES][n % 2]

        for n in range(UNITS + 4):
            if n < UNITS:
                products(n)
            if 2 <= n < UNITS + 2 and maker(n - 2) == "tensor":
                add_bias(n - 2)
            for ahead in range(4) if n == 0 else range(n + 3, n + 4):
                if ahead < UNITS and maker(ahead) == "gpsimd":
                    add_bias(ahead)
            if 1 <= n <= UNITS:
                flip_products(n - 1)
            if 14 <= n < 14 + ROW_TILES:
                close_cell(n - 14)
            if 2 <= n < UNITS and n % 2 == 0:
                quantise_products(n // 2 - 1, slice(0, 2))
            if n == UNITS - 1:
                quantise_products(n // 2, slice(0, 1))
            if n == UNITS:
                quantise_products(n // 2 - 1, slice(1, 2))
            if 3 <= n < UNITS + 3:
                logits(n - 3)
                add(n - 3)
            if n >= 4:
                gate(n - 4)
            if 15 <= n < 15 + ROW_TILES:
                squash_cell(n - 15)
